import numpy as np
import ml_dtypes


def mxq(x, axis, fmt="e4m3"):
    dtype, down = {"e4m3": (ml_dtypes.float8_e4m3fn, 7), "e5m2": (ml_dtypes.float8_e5m2, 14)}[fmt]
    v = np.moveaxis(np.asarray(x, np.float32).astype(ml_dtypes.bfloat16).astype(np.float64), axis, -1)
    blocks = v.reshape(v.shape[:-1] + (-1, 32))
    amax = np.abs(blocks).max(-1, keepdims=True)
    byte = np.maximum(np.where(amax > 0, np.frexp(amax)[1] - 1 + 127, 0) - down, 1)
    scale = np.exp2(byte - 127.0)
    codes = (blocks / scale).astype(np.float32).astype(dtype).astype(np.float64)
    return np.moveaxis((codes * scale).reshape(v.shape), -1, axis)


WIDE = False


def mx_kscale(k):
    if not WIDE:
        return np.ones(k)
    levels = np.array([10, -10, 5, -5, 0])
    a = np.random.permutation(np.resize(levels, k // 512 * 4)).reshape(k // 512, 4)
    idx = np.arange(k)
    return np.exp2(a[idx // 512, idx % 128 // 32])


BF16 = ml_dtypes.bfloat16


def bf(x):
    return np.asarray(x, np.float32).astype(BF16)


def f64(x):
    return np.asarray(x).astype(np.float64)


B, O, P, C, H, D, F = 4, 32, 127, 1024, 16, 64, 4096
N = 1 + O + P
E = H * D
EPS = 1e-5


def layer_norm(t, g, b):
    m = t.mean(-1, keepdims=True)
    v = ((t - m) ** 2).mean(-1, keepdims=True)
    return (t - m) / np.sqrt(v + EPS) * g + b


def qkv_heads(t, w, b):
    y = (mxq(t, 2, "e4m3") @ mxq(w, 0, "e4m3")) + b
    y = y.reshape(t.shape[0], t.shape[1], 3, H, D)
    return [y[:, :, j].transpose(0, 2, 1, 3) for j in range(3)]


def mix(a, p):
    return np.concatenate([a[:, :, :1], p, a[:, :, 1:]], 2)


def setup_inputs():
    s = mx_kscale(C)
    r = np.random.standard_normal
    x = r((B, N, C)) * (0.5 + np.random.random((B, N, 1))) + 0.5 * r((B, N, 1))
    return {"x": bf(x),
            "w_qkv": bf(r((C, 3 * E)) / np.sqrt(C) / s[:, None]), "b_qkv": bf(0.2 * r(3 * E)),
            "w_qkv_p": bf(r((C, 3 * E)) / np.sqrt(C) / s[:, None]), "b_qkv_p": bf(0.2 * r(3 * E)),
            "n1_g": bf((1.0 + 0.1 * r(C)) * s), "n1_b": bf(0.2 * r(C) * s),
            "n1p_g": bf((1.0 + 0.1 * r(C)) * s), "n1p_b": bf(0.2 * r(C) * s)}


def reference(x, w_qkv, b_qkv, w_qkv_p, b_qkv_p, n1_g, n1_b, n1p_g, n1p_b):
    x = f64(x)
    pc = layer_norm(np.concatenate([x[:, :1], x[:, 1 + O:]], 1), f64(n1_g), f64(n1_b))
    pr = layer_norm(x[:, 1:1 + O], f64(n1p_g), f64(n1p_b))
    q_pc, k_pc, v_pc = qkv_heads(pc, f64(w_qkv), f64(b_qkv))
    q_pr, k_pr, v_pr = qkv_heads(pr, f64(w_qkv_p), f64(b_qkv_p))
    return mix(q_pc, q_pr), mix(k_pc, k_pr), mix(v_pc, v_pr)

@@ -1,0 +1,367 @@
+from contextlib import ExitStack
+
+import concourse.mybir as mybir
+from concourse.masks import make_identity
+
+F32 = mybir.dt.float32
+BF16 = mybir.dt.bfloat16
+U32 = mybir.dt.uint32
+U8 = mybir.dt.uint8
+I32 = mybir.dt.int32
+FP8X4 = mybir.dt.float8_e4m3fn_x4
+ACT = mybir.ActivationFunctionType
+ALU = mybir.AluOpType
+
+P = 128
+PACK = 4
+K_PASS = P * PACK
+SAMPLES, TOKENS, WIDTH = 4, 160, 1024
+PROMPTS = 32
+HEADS, HEAD_DIM = 16, 64
+TENSOR_WIDTH = HEADS * HEAD_DIM
+OUT_WIDTH = 3 * TENSOR_WIDTH
+PASSES = WIDTH // K_PASS
+PLANES = WIDTH // P
+EPS = 1e-5
+FLOPS = 2 * SAMPLES * TOKENS * WIDTH * OUT_WIDTH
+
+GROUP = 5
+GROUPS = TOKENS // GROUP
+assert GROUPS * SAMPLES == P
+CHUNK = 512
+CHUNK_HEADS = CHUNK // HEAD_DIM
+CHUNKS = OUT_WIDTH // CHUNK
+
+PATCH, PROMPT = 0, 1
+KINDS = (PROMPT, PATCH)
+SPANS = ((PATCH, 0, 0, 0), (PROMPT, 1, PROMPTS, P), (PATCH, PROMPTS + 1, TOKENS - 1, 1))
+
+VECTOR_COLUMNS = 160
+AHEAD = 3
+UNITS = ((0, PROMPT), (0, PATCH), (1, PROMPT), (1, PATCH))
+
+
+def groups_of(first, last, j):
+    return (first - j + GROUP - 1) // GROUP, (last - j) // GROUP + 1
+
+
+def prompt_columns(j):
+    lo, hi = groups_of(1, PROMPTS, j)
+    return SAMPLES * lo, SAMPLES * hi
+
+def tile_block_pa_kernel(
+    tc, x, w_qkv, b_qkv, w_qkv_p, b_qkv_p, n1_g, n1_b, n1p_g, n1p_b, out_0, out_1, out_2
+):
+    nc = tc.nc
+    weights = {PATCH: w_qkv, PROMPT: w_qkv_p}
+    outs = (out_0, out_1, out_2)
+
+    with ExitStack() as pools:
+        pools.enter_context(tc.manual_schedule())
+        keep = pools.enter_context(tc.tile_pool(name="keep", bufs=1))
+        grouped_pool = pools.enter_context(tc.tile_pool(name="grouped", bufs=AHEAD + 1))
+        codes_pool = pools.enter_context(tc.tile_pool(name="codes", bufs=6))
+        psum = pools.enter_context(tc.psum_pool(name="psum", bufs=8))
+
+        ident = keep.tile([P, P], F32)
+        make_identity(nc, ident[:])
+        x_codes = keep.tile([P, PASSES, GROUP, 2 * P], U32, align_bytes=64)
+        x_scales = keep.tile([P, PASSES, GROUP, 2 * P], U8, align_bytes=64)
+        raw = {}
+        grouped_w = {}
+        bias = {}
+
+        def unit_views(u):
+            chunk, (g, kind) = u // len(UNITS), UNITS[u % len(UNITS)]
+            third, half = divmod(chunk, 2)
+            if u not in grouped_w:
+                grouped_w[u] = grouped_pool.tile([P, CHUNK, PACK], BF16, name="grouped_w", align_bytes=64)
+            source = raw[third, g, kind][:, :, half * CHUNK : (half + 1) * CHUNK]
+            return (
+                source.rearrange("p t (c i) -> p c t i", i=4),
+                grouped_w[u][:].rearrange("p (c i) t -> p c t i", i=4),
+            )
+
+        def regroup_on_vector(u):
+            source, target = unit_views(u)
+            nc.vector.tensor_copy(
+                out=target[:, 0 : VECTOR_COLUMNS // 4], in_=source[:, 0 : VECTOR_COLUMNS // 4]
+            )
+
+        def regroup_on_scalar(u):
+            source, target = unit_views(u)
+            nc.scalar.copy(
+                out=target[:, VECTOR_COLUMNS // 4 : CHUNK // 4],
+                in_=source[:, VECTOR_COLUMNS // 4 : CHUNK // 4],
+            )
+
+        def quantise_and_multiply(u, acc):
+            g, kind = UNITS[u % len(UNITS)]
+            w_codes = codes_pool.tile([P, CHUNK], U32, align_bytes=64)
+            w_scales = codes_pool.tile([P, CHUNK], U8, align_bytes=64)
+            nc.vector.quantize_mx(
+                out=w_codes[:].bitcast(FP8X4),
+                scales=w_scales[:],
+                in_=grouped_w[u][:].rearrange("p c t -> p (c t)"),
+            )
+            for j in range(GROUP):
+                nc.tensor.matmul_mx(
+                    out=acc[j][:],
+                    lhsT=x_codes[:, g, j, kind * P : (kind + 1) * P].bitcast(FP8X4),
+                    lhsT_scale=x_scales[:, g, j, kind * P : (kind + 1) * P],
+                    rhs=w_codes[:].bitcast(FP8X4),
+                    rhs_scale=w_scales[:],
+                    start=(u % len(UNITS) == 0),
+                    stop=(u % len(UNITS) == len(UNITS) - 1),
+                )
+
+        with tc.tile_pool(name="norm", bufs=1) as norm, tc.tile_pool(name="normed", bufs=3) as normed_pool:
+            x_prompt = norm.tile([P, WIDTH], BF16)
+            for b in range(SAMPLES):
+                nc.sync.dma_start(
+                    out=x_prompt[PROMPTS * b : PROMPTS * (b + 1), :], in_=x[b, 1 : 1 + PROMPTS, :]
+                )
+            x_patch = norm.tile([P, SAMPLES, WIDTH], BF16)
+            for b in range(0, SAMPLES, 2):
+                nc.sync.dma_start(
+                    out=x_patch[:, b : b + 2, :],
+                    in_=x[b : b + 2, PROMPTS:TOKENS, :].rearrange("b q c -> q b c"),
+                )
+            x_class = norm.tile([1, SAMPLES, WIDTH], BF16)
+            nc.scalar.dma_start(out=x_class[:], in_=x[:, 0:1, :].rearrange("b o c -> o b c"))
+
+            vector_rows = norm.tile([P, P], BF16)
+            nc.vector.memset(vector_rows[32:64, :], 0.0)
+            nc.vector.memset(vector_rows[64:128, :], 0.0)
+            for v, vector in enumerate((n1_g, n1_b, n1p_g, n1p_b)):
+                nc.scalar.dma_start(
+                    out=vector_rows[PLANES * v : PLANES * (v + 1), :],
+                    in_=vector.rearrange("(r p) -> r p", p=P),
+                )
+            bias_rows = norm.tile([P, OUT_WIDTH], BF16)
+            nc.gpsimd.memset(bias_rows[:].bitcast(F32), 0.0)
+
+            for third in range(3):
+                for g, kind in UNITS:
+                    piece = keep.tile(
+                        [P, PACK, TENSOR_WIDTH], BF16, name="raw_%d_%d_%d" % (third, g, kind)
+                    )
+                    nc.sync.dma_start(
+                        out=piece[:],
+                        in_=weights[kind].rearrange("(g t p) n -> g p t n", t=PACK, p=P)[
+                            g, :, :, third * TENSOR_WIDTH : (third + 1) * TENSOR_WIDTH
+                        ],
+                    )
+                    raw[third, g, kind] = piece
+
+            grouped_x = [
+                norm.tile([P, GROUP, 2, P, PACK], BF16, name="grouped_x_%d" % g, align_bytes=64)
+                for g in range(PASSES)
+            ]
+            for g in range(PASSES):
+                words = grouped_x[g][:].bitcast(I32)
+                nc.vector.memset(words[:, :, PROMPT, :, :], 0)
+                nc.vector.memset(words[:, :, PATCH, 0 : prompt_columns(1)[1], :], 0)
+
+            stats = norm.tile([P, 1 + SAMPLES, 2, 6], F32)
+            mean_var = norm.tile([P, 1 + SAMPLES, 2], F32)
+            minus_half = norm.tile([P, 1], F32)
+            nc.gpsimd.memset(minus_half[:], -0.5)
+            var_eps = norm.tile([P, 1 + SAMPLES], F32)
+            rstd = norm.tile([P, 1 + SAMPLES], F32)
+            minus_mean_rstd = norm.tile([P, 1 + SAMPLES], F32)
+
+            def normalise(a, rows, z):
+                for half in range(2):
+                    nc.vector.bn_stats(
+                        out=stats[:, a, half, :], in_=rows[:, half * K_PASS : (half + 1) * K_PASS]
+                    )
+                nc.vector.bn_aggr(
+                    out=mean_var[:, a, :], in_=stats[:, a, :, :].rearrange("p h s -> p (h s)")
+                )
+                nc.gpsimd.tensor_scalar_add(
+                    out=var_eps[:, a : a + 1], in0=mean_var[:, a, 1:2], scalar1=EPS
+                )
+                nc.gpsimd.tensor_tensor(
+                    out=rstd[:, a : a + 1], in0=var_eps[:, a : a + 1], in1=minus_half[:], op=ALU.pow
+                )
+                nc.gpsimd.tensor_scalar(
+                    out=minus_mean_rstd[:, a : a + 1],
+                    in0=mean_var[:, a, 0:1],
+                    scalar1=rstd[:, a : a + 1],
+                    scalar2=-1.0,
+                    op0=ALU.mult,
+                    op1=ALU.mult,
+                )
+                nc.scalar.activation(
+                    out=z,
+                    in_=rows,
+                    func=ACT.Identity,
+                    scale=rstd[:, a : a + 1],
+                    bias=minus_mean_rstd[:, a : a + 1],
+                )
+
+            z_prompt = norm.tile([P, WIDTH], F32)
+            normalise(0, x_prompt[:], z_prompt[:])
+
+            vector_rows_f32 = norm.tile([P, P], F32)
+            nc.vector.tensor_copy(out=vector_rows_f32[:], in_=vector_rows[:])
+            vector_bank = psum.tile([P, P], F32, tag="bank")
+            nc.tensor.transpose(vector_bank[:], vector_rows_f32[:], ident[:])
+            per_channel = keep.tile([P, 4 * PLANES], F32)
+            gain = {PATCH: per_channel[:, 0:PLANES], PROMPT: per_channel[:, 2 * PLANES : 3 * PLANES]}
+            shift = {
+                PATCH: per_channel[:, PLANES : 2 * PLANES],
+                PROMPT: per_channel[:, 3 * PLANES : 4 * PLANES],
+            }
+
+            patch_banks = []
+            for b in range(SAMPLES):
+                nc.vector.tensor_copy(out=x_patch[0:1, b, :], in_=x_class[0:1, b, :])
+                z_patch = normed_pool.tile([P, WIDTH], F32)
+                normalise(1 + b, x_patch[:, b, :], z_patch[:])
+                if b == 0:
+                    nc.vector.tensor_copy(out=per_channel[:], in_=vector_bank[:, 0 : 4 * PLANES])
+                    for r in range(PLANES):
+                        patch_banks.append(
+                            psum.tile([P, SAMPLES, P], F32, tag="bank", name="patch_bank_%d" % r)
+                        )
+                for r in range(PLANES):
+                    nc.tensor.transpose(
+                        patch_banks[r][:, b, :], z_patch[:, r * P : (r + 1) * P], ident[:]
+                    )
+
+            for u in range(AHEAD):
+                regroup_on_vector(u)
+
+            planes = norm.tile([P, PLANES, TOKENS, SAMPLES], BF16)
+            for t in range(PACK):
+                nc.scalar.activation(
+                    out=planes[:, t, 0:P, :],
+                    in_=patch_banks[t][:].rearrange("p b q -> p q b"),
+                    func=ACT.Identity,
+                    scale=gain[PATCH][:, t : t + 1],
+                    bias=shift[PATCH][:, t : t + 1],
+                )
+                r = PACK + t
+                nc.vector.tensor_scalar(
+                    out=planes[:, r, 0:P, :],
+                    in0=patch_banks[r][:].rearrange("p b q -> p q b"),
+                    scalar1=gain[PATCH][:, r : r + 1],
+                    scalar2=shift[PATCH][:, r : r + 1],
+                    op0=ALU.mult,
+                    op1=ALU.add,
+                )
+            for g in range(PASSES):
+                prompt_bank = psum.tile([P, PACK, P], F32, tag="bank")
+                for t in range(PACK):
+                    r = PACK * g + t
+                    nc.tensor.transpose(
+                        prompt_bank[:, t, :], z_prompt[:, r * P : (r + 1) * P], ident[:]
+                    )
+                for t in range(PACK):
+                    r = PACK * g + t
+                    nc.scalar.activation(
+                        out=planes[:, r, P:TOKENS, :],
+                        in_=prompt_bank[:, t, :].rearrange("p (b m) -> p m b", b=SAMPLES),
+                        func=ACT.Identity,
+                        scale=gain[PROMPT][:, r : r + 1],
+                        bias=shift[PROMPT][:, r : r + 1],
+                    )
+
+            nc.gpsimd.dma_start(out=bias_rows[0:1, :], in_=b_qkv.rearrange("(o n) -> o n", o=1))
+            nc.gpsimd.dma_start(out=bias_rows[32:33, :], in_=b_qkv_p.rearrange("(o n) -> o n", o=1))
+            for j in range(GROUP):
+                columns = prompt_columns(j)
+                if columns not in bias:
+                    lo, hi = columns
+                    pick = norm.tile([P, P], BF16, name="pick_%d" % j)
+                    nc.gpsimd.memset(pick[:], 0.0)
+                    nc.gpsimd.memset(pick[32:64, lo:hi], 1.0)
+                    nc.gpsimd.memset(pick[0:32, hi:P], 1.0)
+                    if lo > 0:
+                        nc.gpsimd.memset(pick[0:32, 0:lo], 1.0)
+                    spread = keep.tile([P, OUT_WIDTH], BF16, name="bias_%d" % j)
+                    for third in range(3):
+                        bias_bank = psum.tile([P, TENSOR_WIDTH], BF16, tag="bank")
+                        for half in range(2):
+                            nc.tensor.matmul(
+                                out=bias_bank[:, half * CHUNK : (half + 1) * CHUNK],
+                                lhsT=pick[:],
+                                rhs=bias_rows[
+                                    :, (2 * third + half) * CHUNK : (2 * third + half + 1) * CHUNK
+                                ],
+                                start=True,
+                                stop=True,
+                            )
+                        nc.scalar.copy(
+                            out=spread[:, third * TENSOR_WIDTH : (third + 1) * TENSOR_WIDTH],
+                            in_=bias_bank[:],
+                        )
+                    bias[columns] = spread
+
+            def regroup_tokens(g, j, wanted):
+                for kind, first, last, slot in SPANS:
+                    lo, hi = groups_of(first, last, j)
+                    if kind == wanted and lo < hi:
+                        s0 = slot + GROUP * lo + j - first
+                        nc.vector.tensor_copy(
+                            out=grouped_x[g][:, j, kind, SAMPLES * lo : SAMPLES * hi, :].rearrange(
+                                "p (i b) t -> p i t b", b=SAMPLES
+                            ),
+                            in_=planes[
+                                :, PACK * g : PACK * (g + 1), s0 : s0 + GROUP * (hi - lo - 1) + 1 : GROUP, :
+                            ].rearrange("p t i b -> p i t b"),
+                        )
+
+            for g in range(PASSES):
+                for j in range(GROUP):
+                    regroup_tokens(g, j, PATCH)
+            for g in range(PASSES):
+                for j in range(GROUP):
+                    regroup_tokens(g, j, PROMPT)
+                    nc.vector.quantize_mx(
+                        out=x_codes[:, g, j, :].bitcast(FP8X4),
+                        scales=x_scales[:, g, j, :],
+                        in_=grouped_x[g][:, j].rearrange("p k c t -> p (k c t)"),
+                    )
+
+            for u in range(AHEAD):
+                regroup_on_scalar(u)
+
+        with tc.tile_pool(name="result", bufs=3) as result_pool:
+
+            def leave_psum(chunk, acc):
+                third, half = divmod(chunk, 2)
+                result = result_pool.tile([P, CHUNK_HEADS, GROUP, HEAD_DIM], F32)
+                for j in range(GROUP):
+                    nc.vector.tensor_tensor(
+                        out=result[:, :, j, :],
+                        in0=acc[j][:].rearrange("p (h d) -> p h d", d=HEAD_DIM),
+                        in1=bias[prompt_columns(j)][:, chunk * CHUNK : (chunk + 1) * CHUNK].rearrange(
+                            "p (h d) -> p h d", d=HEAD_DIM
+                        ),
+                        op=ALU.add,
+                    )
+                for b in range(SAMPLES):
+                    nc.sync.dma_start(
+                        out=outs[third][
+                            b, half * CHUNK_HEADS : (half + 1) * CHUNK_HEADS, :, :
+                        ].rearrange("h (i j) d -> i h (j d)", j=GROUP),
+                        in_=result[b:P:SAMPLES, :, :, :].rearrange("p h j d -> p h (j d)"),
+                    )
+
+            acc = {}
+            for u in range(CHUNKS * len(UNITS)):
+                chunk = u // len(UNITS)
+                if u + AHEAD < CHUNKS * len(UNITS):
+                    regroup_on_scalar(u + AHEAD)
+                    regroup_on_vector(u + AHEAD)
+                if u % len(UNITS) == 0:
+                    acc[chunk] = [
+                        psum.tile([P, CHUNK], F32, tag="bank", name="acc_%d" % j) for j in range(GROUP)
+                    ]
+                quantise_and_multiply(u, acc[chunk])
+                if u % len(UNITS) == 0 and chunk > 0:
+                    leave_psum(chunk - 1, acc[chunk - 1])
+            leave_psum(CHUNKS - 1, acc[CHUNKS - 1])

@@ -37,7 +37,6 @@ KINDS = (PROMPT, PATCH)
 SPANS = ((PATCH, 0, 0, 0), (PROMPT, 1, PROMPTS, P), (PATCH, PROMPTS + 1, TOKENS - 1, 1))
 
 VECTOR_COLUMNS = 160
-AHEAD = 3
 UNITS = ((0, PROMPT), (0, PATCH), (1, PROMPT), (1, PATCH))
 
 
@@ -57,10 +56,9 @@ def tile_block_pa_kernel(
     outs = (out_0, out_1, out_2)
 
     with ExitStack() as pools:
-        pools.enter_context(tc.manual_schedule())
         keep = pools.enter_context(tc.tile_pool(name="keep", bufs=1))
-        grouped_pool = pools.enter_context(tc.tile_pool(name="grouped", bufs=AHEAD + 1))
-        codes_pool = pools.enter_context(tc.tile_pool(name="codes", bufs=6))
+        grouped_pool = pools.enter_context(tc.tile_pool(name="grouped", bufs=4))
+        codes_pool = pools.enter_context(tc.tile_pool(name="codes", bufs=8))
         psum = pools.enter_context(tc.psum_pool(name="psum", bufs=8))
 
         ident = keep.tile([P, P], F32)
@@ -68,65 +66,40 @@ def tile_block_pa_kernel(
         x_codes = keep.tile([P, PASSES, GROUP, 2 * P], U32, align_bytes=64)
         x_scales = keep.tile([P, PASSES, GROUP, 2 * P], U8, align_bytes=64)
         raw = {}
-        grouped_w = {}
+
+        bias_rows = keep.tile([P, OUT_WIDTH], BF16)
+        nc.gpsimd.memset(bias_rows[:].bitcast(F32), 0.0)
+        pick = {}
         bias = {}
+        for j in range(GROUP):
+            columns = prompt_columns(j)
+            if columns not in pick:
+                lo, hi = columns
+                pick[columns] = keep.tile([P, P], BF16, name="pick_%d" % j)
+                bias[columns] = keep.tile([P, OUT_WIDTH], BF16, name="bias_%d" % j)
+                nc.vector.memset(pick[columns][:], 0.0)
+                nc.vector.memset(pick[columns][32:64, lo:hi], 1.0)
+                nc.vector.memset(pick[columns][0:32, hi:P], 1.0)
+                if lo > 0:
+                    nc.vector.memset(pick[columns][0:32, 0:lo], 1.0)
 
-        def unit_views(u):
-            chunk, (g, kind) = u // len(UNITS), UNITS[u % len(UNITS)]
-            third, half = divmod(chunk, 2)
-            if u not in grouped_w:
-                grouped_w[u] = grouped_pool.tile([P, CHUNK, PACK], BF16, name="grouped_w", align_bytes=64)
-            source = raw[third, g, kind][:, :, half * CHUNK : (half + 1) * CHUNK]
-            return (
-                source.rearrange("p t (c i) -> p c t i", i=4),
-                grouped_w[u][:].rearrange("p (c i) t -> p c t i", i=4),
-            )
-
-        def regroup_on_vector(u):
-            source, target = unit_views(u)
-            nc.vector.tensor_copy(
-                out=target[:, 0 : VECTOR_COLUMNS // 4], in_=source[:, 0 : VECTOR_COLUMNS // 4]
-            )
-
-        def regroup_on_scalar(u):
-            source, target = unit_views(u)
-            nc.scalar.copy(
-                out=target[:, VECTOR_COLUMNS // 4 : CHUNK // 4],
-                in_=source[:, VECTOR_COLUMNS // 4 : CHUNK // 4],
-            )
-
-        def quantise_and_multiply(u, acc):
-            g, kind = UNITS[u % len(UNITS)]
-            w_codes = codes_pool.tile([P, CHUNK], U32, align_bytes=64)
-            w_scales = codes_pool.tile([P, CHUNK], U8, align_bytes=64)
-            nc.vector.quantize_mx(
-                out=w_codes[:].bitcast(FP8X4),
-                scales=w_scales[:],
-                in_=grouped_w[u][:].rearrange("p c t -> p (c t)"),
-            )
-            for j in range(GROUP):
-                nc.tensor.matmul_mx(
-                    out=acc[j][:],
-                    lhsT=x_codes[:, g, j, kind * P : (kind + 1) * P].bitcast(FP8X4),
-                    lhsT_scale=x_scales[:, g, j, kind * P : (kind + 1) * P],
-                    rhs=w_codes[:].bitcast(FP8X4),
-                    rhs_scale=w_scales[:],
-                    start=(u % len(UNITS) == 0),
-                    stop=(u % len(UNITS) == len(UNITS) - 1),
+        def spread_bias(third):
+            for columns in pick:
+                bias_bank = psum.tile([P, TENSOR_WIDTH], BF16, tag="bank")
+                for half in range(2):
+                    nc.tensor.matmul(
+                        out=bias_bank[:, half * CHUNK : (half + 1) * CHUNK],
+                        lhsT=pick[columns][:],
+                        rhs=bias_rows[:, (2 * third + half) * CHUNK : (2 * third + half + 1) * CHUNK],
+                        start=True,
+                        stop=True,
+                    )
+                nc.scalar.copy(
+                    out=bias[columns][:, third * TENSOR_WIDTH : (third + 1) * TENSOR_WIDTH],
+                    in_=bias_bank[:],
                 )
 
         with tc.tile_pool(name="norm", bufs=1) as norm, tc.tile_pool(name="normed", bufs=3) as normed_pool:
-            x_prompt = norm.tile([P, WIDTH], BF16)
-            for b in range(SAMPLES):
-                nc.sync.dma_start(
-                    out=x_prompt[PROMPTS * b : PROMPTS * (b + 1), :], in_=x[b, 1 : 1 + PROMPTS, :]
-                )
-            x_patch = norm.tile([P, SAMPLES, WIDTH], BF16)
-            for b in range(0, SAMPLES, 2):
-                nc.sync.dma_start(
-                    out=x_patch[:, b : b + 2, :],
-                    in_=x[b : b + 2, PROMPTS:TOKENS, :].rearrange("b q c -> q b c"),
-                )
             x_class = norm.tile([1, SAMPLES, WIDTH], BF16)
             nc.scalar.dma_start(out=x_class[:], in_=x[:, 0:1, :].rearrange("b o c -> o b c"))
 
@@ -138,9 +111,20 @@ def tile_block_pa_kernel(
                     out=vector_rows[PLANES * v : PLANES * (v + 1), :],
                     in_=vector.rearrange("(r p) -> r p", p=P),
                 )
-            bias_rows = norm.tile([P, OUT_WIDTH], BF16)
-            nc.gpsimd.memset(bias_rows[:].bitcast(F32), 0.0)
+            nc.scalar.dma_start(out=bias_rows[0:1, :], in_=b_qkv.rearrange("(o n) -> o n", o=1))
+            nc.scalar.dma_start(out=bias_rows[32:33, :], in_=b_qkv_p.rearrange("(o n) -> o n", o=1))
 
+            x_prompt = norm.tile([P, WIDTH], BF16)
+            for b in range(SAMPLES):
+                nc.sync.dma_start(
+                    out=x_prompt[PROMPTS * b : PROMPTS * (b + 1), :], in_=x[b, 1 : 1 + PROMPTS, :]
+                )
+            x_patch = norm.tile([P, SAMPLES, WIDTH], BF16)
+            for b in range(0, SAMPLES, 2):
+                nc.sync.dma_start(
+                    out=x_patch[:, b : b + 2, :],
+                    in_=x[b : b + 2, PROMPTS:TOKENS, :].rearrange("b q c -> q b c"),
+                )
             for third in range(3):
                 for g, kind in UNITS:
                     piece = keep.tile(
@@ -201,57 +185,22 @@ def tile_block_pa_kernel(
                     bias=minus_mean_rstd[:, a : a + 1],
                 )
 
-            z_prompt = norm.tile([P, WIDTH], F32)
-            normalise(0, x_prompt[:], z_prompt[:])
-
             vector_rows_f32 = norm.tile([P, P], F32)
             nc.vector.tensor_copy(out=vector_rows_f32[:], in_=vector_rows[:])
             vector_bank = psum.tile([P, P], F32, tag="bank")
             nc.tensor.transpose(vector_bank[:], vector_rows_f32[:], ident[:])
             per_channel = keep.tile([P, 4 * PLANES], F32)
+            nc.vector.tensor_copy(out=per_channel[:], in_=vector_bank[:, 0 : 4 * PLANES])
             gain = {PATCH: per_channel[:, 0:PLANES], PROMPT: per_channel[:, 2 * PLANES : 3 * PLANES]}
             shift = {
                 PATCH: per_channel[:, PLANES : 2 * PLANES],
                 PROMPT: per_channel[:, 3 * PLANES : 4 * PLANES],
             }
 
-            patch_banks = []
-            for b in range(SAMPLES):
-                nc.vector.tensor_copy(out=x_patch[0:1, b, :], in_=x_class[0:1, b, :])
-                z_patch = normed_pool.tile([P, WIDTH], F32)
-                normalise(1 + b, x_patch[:, b, :], z_patch[:])
-                if b == 0:
-                    nc.vector.tensor_copy(out=per_channel[:], in_=vector_bank[:, 0 : 4 * PLANES])
-                    for r in range(PLANES):
-                        patch_banks.append(
-                            psum.tile([P, SAMPLES, P], F32, tag="bank", name="patch_bank_%d" % r)
-                        )
-                for r in range(PLANES):
-                    nc.tensor.transpose(
-                        patch_banks[r][:, b, :], z_patch[:, r * P : (r + 1) * P], ident[:]
-                    )
-
-            for u in range(AHEAD):
-                regroup_on_vector(u)
-
             planes = norm.tile([P, PLANES, TOKENS, SAMPLES], BF16)
-            for t in range(PACK):
-                nc.scalar.activation(
-                    out=planes[:, t, 0:P, :],
-                    in_=patch_banks[t][:].rearrange("p b q -> p q b"),
-                    func=ACT.Identity,
-                    scale=gain[PATCH][:, t : t + 1],
-                    bias=shift[PATCH][:, t : t + 1],
-                )
-                r = PACK + t
-                nc.vector.tensor_scalar(
-                    out=planes[:, r, 0:P, :],
-                    in0=patch_banks[r][:].rearrange("p b q -> p q b"),
-                    scalar1=gain[PATCH][:, r : r + 1],
-                    scalar2=shift[PATCH][:, r : r + 1],
-                    op0=ALU.mult,
-                    op1=ALU.add,
-                )
+
+            z_prompt = normed_pool.tile([P, WIDTH], F32, name="z")
+            normalise(0, x_prompt[:], z_prompt[:])
             for g in range(PASSES):
                 prompt_bank = psum.tile([P, PACK, P], F32, tag="bank")
                 for t in range(PACK):
@@ -261,78 +210,93 @@ def tile_block_pa_kernel(
                     )
                 for t in range(PACK):
                     r = PACK * g + t
-                    nc.scalar.activation(
+                    nc.vector.tensor_scalar(
                         out=planes[:, r, P:TOKENS, :],
-                        in_=prompt_bank[:, t, :].rearrange("p (b m) -> p m b", b=SAMPLES),
-                        func=ACT.Identity,
-                        scale=gain[PROMPT][:, r : r + 1],
-                        bias=shift[PROMPT][:, r : r + 1],
+                        in0=prompt_bank[:, t, :].rearrange("p (b m) -> p m b", b=SAMPLES),
+                        scalar1=gain[PROMPT][:, r : r + 1],
+                        scalar2=shift[PROMPT][:, r : r + 1],
+                        op0=ALU.mult,
+                        op1=ALU.add,
                     )
 
-            nc.gpsimd.dma_start(out=bias_rows[0:1, :], in_=b_qkv.rearrange("(o n) -> o n", o=1))
-            nc.gpsimd.dma_start(out=bias_rows[32:33, :], in_=b_qkv_p.rearrange("(o n) -> o n", o=1))
-            for j in range(GROUP):
-                columns = prompt_columns(j)
-                if columns not in bias:
-                    lo, hi = columns
-                    pick = norm.tile([P, P], BF16, name="pick_%d" % j)
-                    nc.gpsimd.memset(pick[:], 0.0)
-                    nc.gpsimd.memset(pick[32:64, lo:hi], 1.0)
-                    nc.gpsimd.memset(pick[0:32, hi:P], 1.0)
-                    if lo > 0:
-                        nc.gpsimd.memset(pick[0:32, 0:lo], 1.0)
-                    spread = keep.tile([P, OUT_WIDTH], BF16, name="bias_%d" % j)
-                    for third in range(3):
-                        bias_bank = psum.tile([P, TENSOR_WIDTH], BF16, tag="bank")
-                        for half in range(2):
-                            nc.tensor.matmul(
-                                out=bias_bank[:, half * CHUNK : (half + 1) * CHUNK],
-                                lhsT=pick[:],
-                                rhs=bias_rows[
-                                    :, (2 * third + half) * CHUNK : (2 * third + half + 1) * CHUNK
-                                ],
-                                start=True,
-                                stop=True,
+            patch_banks = [
+                psum.tile([P, SAMPLES, P], F32, tag="bank", name="patch_bank_%d" % r)
+                for r in range(PLANES)
+            ]
+            for b in range(SAMPLES):
+                nc.vector.tensor_copy(out=x_patch[0:1, b, :], in_=x_class[0:1, b, :])
+                z_patch = normed_pool.tile([P, WIDTH], F32, name="z")
+                normalise(1 + b, x_patch[:, b, :], z_patch[:])
+                for r in range(PLANES):
+                    nc.tensor.transpose(
+                        patch_banks[r][:, b, :], z_patch[:, r * P : (r + 1) * P], ident[:]
+                    )
+            for r in range(PLANES):
+                nc.scalar.activation(
+                    out=planes[:, r, 0:P, :],
+                    in_=patch_banks[r][:].rearrange("p b q -> p q b"),
+                    func=ACT.Identity,
+                    scale=gain[PATCH][:, r : r + 1],
+                    bias=shift[PATCH][:, r : r + 1],
+                )
+
+            for g in range(PASSES):
+                for j in range(GROUP):
+                    for kind, first, last, slot in SPANS:
+                        lo, hi = groups_of(first, last, j)
+                        if lo < hi:
+                            s0 = slot + GROUP * lo + j - first
+                            nc.vector.tensor_copy(
+                                out=grouped_x[g][:, j, kind, SAMPLES * lo : SAMPLES * hi, :].rearrange(
+                                    "p (i b) t -> p i t b", b=SAMPLES
+                                ),
+                                in_=planes[
+                                    :, PACK * g : PACK * (g + 1), s0 : s0 + GROUP * (hi - lo - 1) + 1 : GROUP, :
+                                ].rearrange("p t i b -> p i t b"),
                             )
-                        nc.scalar.copy(
-                            out=spread[:, third * TENSOR_WIDTH : (third + 1) * TENSOR_WIDTH],
-                            in_=bias_bank[:],
-                        )
-                    bias[columns] = spread
-
-            def regroup_tokens(g, j, wanted):
-                for kind, first, last, slot in SPANS:
-                    lo, hi = groups_of(first, last, j)
-                    if kind == wanted and lo < hi:
-                        s0 = slot + GROUP * lo + j - first
-                        nc.vector.tensor_copy(
-                            out=grouped_x[g][:, j, kind, SAMPLES * lo : SAMPLES * hi, :].rearrange(
-                                "p (i b) t -> p i t b", b=SAMPLES
-                            ),
-                            in_=planes[
-                                :, PACK * g : PACK * (g + 1), s0 : s0 + GROUP * (hi - lo - 1) + 1 : GROUP, :
-                            ].rearrange("p t i b -> p i t b"),
-                        )
-
-            for g in range(PASSES):
-                for j in range(GROUP):
-                    regroup_tokens(g, j, PATCH)
-            for g in range(PASSES):
-                for j in range(GROUP):
-                    regroup_tokens(g, j, PROMPT)
                     nc.vector.quantize_mx(
                         out=x_codes[:, g, j, :].bitcast(FP8X4),
                         scales=x_scales[:, g, j, :],
                         in_=grouped_x[g][:, j].rearrange("p k c t -> p (k c t)"),
                     )
 
-            for u in range(AHEAD):
-                regroup_on_scalar(u)
-
         with tc.tile_pool(name="result", bufs=3) as result_pool:
-
-            def leave_psum(chunk, acc):
+            for chunk in range(CHUNKS):
                 third, half = divmod(chunk, 2)
+                acc = [
+                    psum.tile([P, CHUNK], F32, tag="bank", name="acc_%d" % j) for j in range(GROUP)
+                ]
+                for g, kind in UNITS:
+                    source = raw[third, g, kind][:, :, half * CHUNK : (half + 1) * CHUNK]
+                    grouped_w = grouped_pool.tile([P, CHUNK, PACK], BF16, align_bytes=64)
+                    nc.vector.tensor_copy(
+                        out=grouped_w[:, 0:VECTOR_COLUMNS, :].rearrange("p (c i) t -> p c t i", i=4),
+                        in_=source[:, :, 0:VECTOR_COLUMNS].rearrange("p t (c i) -> p c t i", i=4),
+                    )
+                    nc.scalar.copy(
+                        out=grouped_w[:, VECTOR_COLUMNS:CHUNK, :].rearrange("p (c i) t -> p c t i", i=4),
+                        in_=source[:, :, VECTOR_COLUMNS:CHUNK].rearrange("p t (c i) -> p c t i", i=4),
+                    )
+                    w_codes = codes_pool.tile([P, CHUNK], U32, align_bytes=64)
+                    w_scales = codes_pool.tile([P, CHUNK], U8, align_bytes=64)
+                    nc.vector.quantize_mx(
+                        out=w_codes[:].bitcast(FP8X4),
+                        scales=w_scales[:],
+                        in_=grouped_w[:].rearrange("p c t -> p (c t)"),
+                    )
+                    for j in range(GROUP):
+                        nc.tensor.matmul_mx(
+                            out=acc[j][:],
+                            lhsT=x_codes[:, g, j, kind * P : (kind + 1) * P].bitcast(FP8X4),
+                            lhsT_scale=x_scales[:, g, j, kind * P : (kind + 1) * P],
+                            rhs=w_codes[:].bitcast(FP8X4),
+                            rhs_scale=w_scales[:],
+                            start=((g, kind) == UNITS[0]),
+                            stop=((g, kind) == UNITS[-1]),
+                        )
+
+                if half == 0:
+                    spread_bias(third)
                 result = result_pool.tile([P, CHUNK_HEADS, GROUP, HEAD_DIM], F32)
                 for j in range(GROUP):
                     nc.vector.tensor_tensor(
@@ -350,18 +314,3 @@ def tile_block_pa_kernel(
                         ].rearrange("h (i j) d -> i h (j d)", j=GROUP),
                         in_=result[b:P:SAMPLES, :, :, :].rearrange("p h j d -> p h (j d)"),
                     )
-
-            acc = {}
-            for u in range(CHUNKS * len(UNITS)):
-                chunk = u // len(UNITS)
-                if u + AHEAD < CHUNKS * len(UNITS):
-                    regroup_on_scalar(u + AHEAD)
-                    regroup_on_vector(u + AHEAD)
-                if u % len(UNITS) == 0:
-                    acc[chunk] = [
-                        psum.tile([P, CHUNK], F32, tag="bank", name="acc_%d" % j) for j in range(GROUP)
-                    ]
-                quantise_and_multiply(u, acc[chunk])
-                if u % len(UNITS) == 0 and chunk > 0:
-                    leave_psum(chunk - 1, acc[chunk - 1])
-            leave_psum(CHUNKS - 1, acc[CHUNKS - 1])

@@ -7,7 +7,6 @@ F32 = mybir.dt.float32
 BF16 = mybir.dt.bfloat16
 U32 = mybir.dt.uint32
 U8 = mybir.dt.uint8
-I32 = mybir.dt.int32
 FP8X4 = mybir.dt.float8_e4m3fn_x4
 ACT = mybir.ActivationFunctionType
 ALU = mybir.AluOpType
@@ -25,28 +24,21 @@ PLANES = WIDTH // P
 EPS = 1e-5
 FLOPS = 2 * SAMPLES * TOKENS * WIDTH * OUT_WIDTH
 
-GROUP = 5
-GROUPS = TOKENS // GROUP
-assert GROUPS * SAMPLES == P
+TILES = 4
 CHUNK = 512
 CHUNK_HEADS = CHUNK // HEAD_DIM
 CHUNKS = OUT_WIDTH // CHUNK
 
 PATCH, PROMPT = 0, 1
-KINDS = (PROMPT, PATCH)
-SPANS = ((PATCH, 0, 0, 0), (PROMPT, 1, PROMPTS, P), (PATCH, PROMPTS + 1, TOKENS - 1, 1))
 
-VECTOR_COLUMNS = 160
-UNITS = ((0, PROMPT), (0, PATCH), (1, PROMPT), (1, PATCH))
+KINDS = (PATCH, PROMPT)
+UNITS = 2 * CHUNKS * PASSES
+UNIT_KIND = [PATCH] * (CHUNKS * PASSES) + [PROMPT] * (CHUNKS * PASSES)
+PIECES = {PATCH: ((0, 1), (1, 2), (3, 3)), PROMPT: ((0, 3), (3, 3))}
 
+HEAD_UNITS = 4
+VECTOR_COLUMNS = [256] * HEAD_UNITS + [48] * (CHUNKS * PASSES - HEAD_UNITS) + [128] * (CHUNKS * PASSES)
 
-def groups_of(first, last, j):
-    return (first - j + GROUP - 1) // GROUP, (last - j) // GROUP + 1
-
-
-def prompt_columns(j):
-    lo, hi = groups_of(1, PROMPTS, j)
-    return SAMPLES * lo, SAMPLES * hi
 
 def tile_block_pa_kernel(
     tc, x, w_qkv, b_qkv, w_qkv_p, b_qkv_p, n1_g, n1_b, n1p_g, n1p_b, out_0, out_1, out_2
@@ -57,260 +49,349 @@ def tile_block_pa_kernel(
 
     with ExitStack() as pools:
         keep = pools.enter_context(tc.tile_pool(name="keep", bufs=1))
-        grouped_pool = pools.enter_context(tc.tile_pool(name="grouped", bufs=4))
+        z_pool = pools.enter_context(tc.tile_pool(name="z", bufs=3))
+        grouped_pool = pools.enter_context(tc.tile_pool(name="grouped", bufs=5))
         codes_pool = pools.enter_context(tc.tile_pool(name="codes", bufs=8))
+        result_pool = pools.enter_context(tc.tile_pool(name="result", bufs=3))
         psum = pools.enter_context(tc.psum_pool(name="psum", bufs=8))
+        pools.enter_context(tc.manual_schedule())
 
+        minus_half = keep.tile([P, 2], F32)
+        scratch = keep.tile([P, 2], F32)
+        bias_rows = keep.tile([P, OUT_WIDTH], BF16)
         ident = keep.tile([P, P], F32)
-        make_identity(nc, ident[:])
-        x_codes = keep.tile([P, PASSES, GROUP, 2 * P], U32, align_bytes=64)
-        x_scales = keep.tile([P, PASSES, GROUP, 2 * P], U8, align_bytes=64)
+        x_class = keep.tile([SAMPLES, WIDTH], BF16)
+        vectors = keep.tile([P, 4, 2 * PLANES], BF16)
+        gain_shift = keep.tile([P, 4, PLANES], F32)
+        x_patch = keep.tile([P, TILES, WIDTH], BF16)
+        x_prompt = keep.tile([P, WIDTH], BF16)
+        stats = keep.tile([P, TILES + 1, 2, 6], F32)
+        mean_var = keep.tile([P, TILES + 1, 2], F32)
+        var_eps = keep.tile([P, TILES + 1], F32)
+        rstd = keep.tile([P, TILES + 1], F32)
+        minus_mean = keep.tile([P, TILES + 1], F32)
+        minus_mean_rstd = keep.tile([P, TILES + 1], F32)
+        x_planes = keep.tile([P, PLANES, TILES * P], BF16)
+        x_codes = keep.tile([P, PASSES, TILES * P], U32, align_bytes=64)
+        x_scales = keep.tile([P, PASSES, TILES * P], U8, align_bytes=64)
+        p_planes = keep.tile([P, PLANES, P], BF16)
+        p_grouped = keep.tile([P, PASSES, P, PACK], BF16, align_bytes=64)
+        p_codes = keep.tile([P, PASSES, P], U32, align_bytes=64)
+        p_scales = keep.tile([P, PASSES, P], U8, align_bytes=64)
+
+        def load_patch(j):
+            for b in range(SAMPLES):
+                nc.sync.dma_start(
+                    out=x_patch[b:P:SAMPLES, j : j + 2, :],
+                    in_=x[b, PROMPTS:TOKENS, :].rearrange("(i j) c -> i j c", j=TILES)[
+                        :, j : j + 2, :
+                    ],
+                )
+
         raw = {}
 
-        bias_rows = keep.tile([P, OUT_WIDTH], BF16)
-        nc.gpsimd.memset(bias_rows[:].bitcast(F32), 0.0)
+        def load_piece(kind, which, g):
+            first, chunks = PIECES[kind][which]
+            piece = keep.tile([P, PACK, chunks * CHUNK], BF16, name="raw_%d_%d_%d" % (kind, which, g))
+            nc.sync.dma_start(
+                out=piece[:],
+                in_=weights[kind].rearrange("(g p t) n -> g p t n", p=P, t=PACK)[
+                    g, :, :, first * CHUNK : (first + chunks) * CHUNK
+                ],
+            )
+            for c in range(chunks):
+                raw[kind, first + c, g] = piece[:, :, c * CHUNK : (c + 1) * CHUNK]
+
         pick = {}
         bias = {}
-        for j in range(GROUP):
-            columns = prompt_columns(j)
-            if columns not in pick:
-                lo, hi = columns
-                pick[columns] = keep.tile([P, P], BF16, name="pick_%d" % j)
-                bias[columns] = keep.tile([P, OUT_WIDTH], BF16, name="bias_%d" % j)
-                nc.vector.memset(pick[columns][:], 0.0)
-                nc.vector.memset(pick[columns][32:64, lo:hi], 1.0)
-                nc.vector.memset(pick[columns][0:32, hi:P], 1.0)
-                if lo > 0:
-                    nc.vector.memset(pick[columns][0:32, 0:lo], 1.0)
 
-        def spread_bias(third):
-            for columns in pick:
-                bias_bank = psum.tile([P, TENSOR_WIDTH], BF16, tag="bank")
+        def spread_bias(kind):
+            for third in range(3):
+                bank = psum.tile([P, TENSOR_WIDTH], BF16, tag="bank", name="bias_bank")
                 for half in range(2):
+                    first = third * TENSOR_WIDTH + half * CHUNK
                     nc.tensor.matmul(
-                        out=bias_bank[:, half * CHUNK : (half + 1) * CHUNK],
-                        lhsT=pick[columns][:],
-                        rhs=bias_rows[:, (2 * third + half) * CHUNK : (2 * third + half + 1) * CHUNK],
+                        out=bank[:, half * CHUNK : (half + 1) * CHUNK],
+                        lhsT=pick[kind][:],
+                        rhs=bias_rows[:, first : first + CHUNK],
                         start=True,
                         stop=True,
                     )
                 nc.scalar.copy(
-                    out=bias[columns][:, third * TENSOR_WIDTH : (third + 1) * TENSOR_WIDTH],
-                    in_=bias_bank[:],
+                    out=bias[kind][:, third * TENSOR_WIDTH : (third + 1) * TENSOR_WIDTH], in_=bank[:]
                 )
 
-        with tc.tile_pool(name="norm", bufs=1) as norm, tc.tile_pool(name="normed", bufs=3) as normed_pool:
-            x_class = norm.tile([1, SAMPLES, WIDTH], BF16)
-            nc.scalar.dma_start(out=x_class[:], in_=x[:, 0:1, :].rearrange("b o c -> o b c"))
+        def statistics(a, rows):
+            for half in range(2):
+                nc.vector.bn_stats(
+                    out=stats[:, a, half, :], in_=rows[:, half * K_PASS : (half + 1) * K_PASS]
+                )
+            nc.vector.bn_aggr(
+                out=mean_var[:, a, :], in_=stats[:, a, :, :].rearrange("p h s -> p (h s)")
+            )
 
-            vector_rows = norm.tile([P, P], BF16)
-            nc.vector.memset(vector_rows[32:64, :], 0.0)
-            nc.vector.memset(vector_rows[64:128, :], 0.0)
-            for v, vector in enumerate((n1_g, n1_b, n1p_g, n1p_b)):
-                nc.scalar.dma_start(
-                    out=vector_rows[PLANES * v : PLANES * (v + 1), :],
-                    in_=vector.rearrange("(r p) -> r p", p=P),
-                )
-            nc.scalar.dma_start(out=bias_rows[0:1, :], in_=b_qkv.rearrange("(o n) -> o n", o=1))
-            nc.scalar.dma_start(out=bias_rows[32:33, :], in_=b_qkv_p.rearrange("(o n) -> o n", o=1))
+        def scales(lo, hi):
+            nc.vector.tensor_scalar_add(
+                out=var_eps[:, lo:hi], in0=mean_var[:, lo:hi, 1], scalar1=EPS
+            )
+            nc.vector.tensor_scalar_mul(
+                out=minus_mean[:, lo:hi], in0=mean_var[:, lo:hi, 0], scalar1=-1.0
+            )
+            nc.gpsimd.tensor_tensor(
+                out=rstd[:, lo:hi], in0=var_eps[:, lo:hi], in1=minus_half[:, 0 : hi - lo], op=ALU.pow
+            )
+            nc.gpsimd.tensor_tensor(
+                out=minus_mean_rstd[:, lo:hi], in0=minus_mean[:, lo:hi], in1=rstd[:, lo:hi], op=ALU.mult
+            )
 
-            x_prompt = norm.tile([P, WIDTH], BF16)
-            for b in range(SAMPLES):
-                nc.sync.dma_start(
-                    out=x_prompt[PROMPTS * b : PROMPTS * (b + 1), :], in_=x[b, 1 : 1 + PROMPTS, :]
-                )
-            x_patch = norm.tile([P, SAMPLES, WIDTH], BF16)
-            for b in range(0, SAMPLES, 2):
-                nc.sync.dma_start(
-                    out=x_patch[:, b : b + 2, :],
-                    in_=x[b : b + 2, PROMPTS:TOKENS, :].rearrange("b q c -> q b c"),
-                )
-            for third in range(3):
-                for g, kind in UNITS:
-                    piece = keep.tile(
-                        [P, PACK, TENSOR_WIDTH], BF16, name="raw_%d_%d_%d" % (third, g, kind)
-                    )
-                    nc.sync.dma_start(
-                        out=piece[:],
-                        in_=weights[kind].rearrange("(g t p) n -> g p t n", t=PACK, p=P)[
-                            g, :, :, third * TENSOR_WIDTH : (third + 1) * TENSOR_WIDTH
-                        ],
-                    )
-                    raw[third, g, kind] = piece
-
-            grouped_x = [
-                norm.tile([P, GROUP, 2, P, PACK], BF16, name="grouped_x_%d" % g, align_bytes=64)
-                for g in range(PASSES)
-            ]
-            for g in range(PASSES):
-                words = grouped_x[g][:].bitcast(I32)
-                nc.vector.memset(words[:, :, PROMPT, :, :], 0)
-                nc.vector.memset(words[:, :, PATCH, 0 : prompt_columns(1)[1], :], 0)
-
-            stats = norm.tile([P, 1 + SAMPLES, 2, 6], F32)
-            mean_var = norm.tile([P, 1 + SAMPLES, 2], F32)
-            minus_half = norm.tile([P, 1], F32)
-            nc.gpsimd.memset(minus_half[:], -0.5)
-            var_eps = norm.tile([P, 1 + SAMPLES], F32)
-            rstd = norm.tile([P, 1 + SAMPLES], F32)
-            minus_mean_rstd = norm.tile([P, 1 + SAMPLES], F32)
-
-            def normalise(a, rows, z):
-                for half in range(2):
-                    nc.vector.bn_stats(
-                        out=stats[:, a, half, :], in_=rows[:, half * K_PASS : (half + 1) * K_PASS]
-                    )
-                nc.vector.bn_aggr(
-                    out=mean_var[:, a, :], in_=stats[:, a, :, :].rearrange("p h s -> p (h s)")
-                )
-                nc.gpsimd.tensor_scalar_add(
-                    out=var_eps[:, a : a + 1], in0=mean_var[:, a, 1:2], scalar1=EPS
-                )
-                nc.gpsimd.tensor_tensor(
-                    out=rstd[:, a : a + 1], in0=var_eps[:, a : a + 1], in1=minus_half[:], op=ALU.pow
-                )
-                nc.gpsimd.tensor_scalar(
-                    out=minus_mean_rstd[:, a : a + 1],
-                    in0=mean_var[:, a, 0:1],
-                    scalar1=rstd[:, a : a + 1],
-                    scalar2=-1.0,
-                    op0=ALU.mult,
-                    op1=ALU.mult,
-                )
+        def normalise(a, rows, on_scalar):
+            z = z_pool.tile([P, PLANES, P], F32, name="z")
+            out = z[:].rearrange("q (g t) p -> q g t p", t=PACK)
+            in_ = rows.rearrange("q (g p t) -> q g t p", p=P, t=PACK)
+            if on_scalar:
                 nc.scalar.activation(
-                    out=z,
-                    in_=rows,
+                    out=out,
+                    in_=in_,
                     func=ACT.Identity,
                     scale=rstd[:, a : a + 1],
                     bias=minus_mean_rstd[:, a : a + 1],
                 )
+            else:
+                nc.gpsimd.tensor_scalar(
+                    out=out,
+                    in0=in_,
+                    scalar1=rstd[:, a : a + 1],
+                    scalar2=minus_mean_rstd[:, a : a + 1],
+                    op0=ALU.mult,
+                    op1=ALU.add,
+                )
+            return z
 
-            vector_rows_f32 = norm.tile([P, P], F32)
-            nc.vector.tensor_copy(out=vector_rows_f32[:], in_=vector_rows[:])
-            vector_bank = psum.tile([P, P], F32, tag="bank")
-            nc.tensor.transpose(vector_bank[:], vector_rows_f32[:], ident[:])
-            per_channel = keep.tile([P, 4 * PLANES], F32)
-            nc.vector.tensor_copy(out=per_channel[:], in_=vector_bank[:, 0 : 4 * PLANES])
-            gain = {PATCH: per_channel[:, 0:PLANES], PROMPT: per_channel[:, 2 * PLANES : 3 * PLANES]}
-            shift = {
-                PATCH: per_channel[:, PLANES : 2 * PLANES],
-                PROMPT: per_channel[:, 3 * PLANES : 4 * PLANES],
-            }
+        def gain_on_scalar(out, bank, vector, r):
+            nc.scalar.activation(
+                out=out,
+                in_=bank,
+                func=ACT.Identity,
+                scale=gain_shift[:, vector, r : r + 1],
+                bias=gain_shift[:, vector + 1, r : r + 1],
+            )
 
-            planes = norm.tile([P, PLANES, TOKENS, SAMPLES], BF16)
+        def gain_on_vector(out, bank, vector, r):
+            nc.vector.tensor_scalar(
+                out=out,
+                in0=bank,
+                scalar1=gain_shift[:, vector, r : r + 1],
+                scalar2=gain_shift[:, vector + 1, r : r + 1],
+                op0=ALU.mult,
+                op1=ALU.add,
+            )
 
-            z_prompt = normed_pool.tile([P, WIDTH], F32, name="z")
-            normalise(0, x_prompt[:], z_prompt[:])
-            for g in range(PASSES):
-                prompt_bank = psum.tile([P, PACK, P], F32, tag="bank")
-                for t in range(PACK):
-                    r = PACK * g + t
-                    nc.tensor.transpose(
-                        prompt_bank[:, t, :], z_prompt[:, r * P : (r + 1) * P], ident[:]
+        def interleave(dst, src, columns, vector_columns):
+            for copy, lo, hi in (
+                (nc.scalar.copy, vector_columns, columns),
+                (nc.vector.tensor_copy, 0, vector_columns),
+            ):
+                if lo < hi:
+                    copy(
+                        out=dst[:, lo:hi, :].rearrange("p (c i) t -> p c t i", i=4),
+                        in_=src[:, :, lo:hi].rearrange("p t (c i) -> p c t i", i=4),
                     )
-                for t in range(PACK):
-                    r = PACK * g + t
-                    nc.vector.tensor_scalar(
-                        out=planes[:, r, P:TOKENS, :],
-                        in0=prompt_bank[:, t, :].rearrange("p (b m) -> p m b", b=SAMPLES),
-                        scalar1=gain[PROMPT][:, r : r + 1],
-                        scalar2=shift[PROMPT][:, r : r + 1],
-                        op0=ALU.mult,
-                        op1=ALU.add,
-                    )
 
-            patch_banks = [
-                psum.tile([P, SAMPLES, P], F32, tag="bank", name="patch_bank_%d" % r)
-                for r in range(PLANES)
-            ]
-            for b in range(SAMPLES):
-                nc.vector.tensor_copy(out=x_patch[0:1, b, :], in_=x_class[0:1, b, :])
-                z_patch = normed_pool.tile([P, WIDTH], F32, name="z")
-                normalise(1 + b, x_patch[:, b, :], z_patch[:])
-                for r in range(PLANES):
-                    nc.tensor.transpose(
-                        patch_banks[r][:, b, :], z_patch[:, r * P : (r + 1) * P], ident[:]
-                    )
-            for r in range(PLANES):
-                nc.scalar.activation(
-                    out=planes[:, r, 0:P, :],
-                    in_=patch_banks[r][:].rearrange("p b q -> p q b"),
-                    func=ACT.Identity,
-                    scale=gain[PATCH][:, r : r + 1],
-                    bias=shift[PATCH][:, r : r + 1],
+        grouped = {}
+        w_operand = {}
+
+        def interleave_unit(u):
+            if u < UNITS:
+                chunk, g = divmod(u % (CHUNKS * PASSES), PASSES)
+                grouped[u] = grouped_pool.tile(
+                    [P, CHUNK, PACK], BF16, name="grouped", align_bytes=64
+                )
+                interleave(grouped[u], raw[UNIT_KIND[u], chunk, g], CHUNK, VECTOR_COLUMNS[u])
+
+        def quantise_unit(u):
+            if u < UNITS:
+                w_codes = codes_pool.tile([P, CHUNK], U32, name="w_codes", align_bytes=64)
+                w_scales = codes_pool.tile([P, CHUNK], U8, name="w_scales", align_bytes=64)
+                nc.vector.quantize_mx(
+                    out=w_codes[:].bitcast(FP8X4),
+                    scales=w_scales[:],
+                    in_=grouped[u][:].rearrange("p c t -> p (c t)"),
+                )
+                w_operand[u] = (w_codes, w_scales)
+
+        acc = {}
+
+        def multiply_unit(u):
+            kind = UNIT_KIND[u]
+            chunk, g = divmod(u, PASSES)
+            codes, code_scales, tiles = (
+                (x_codes, x_scales, TILES) if kind == PATCH else (p_codes, p_scales, 1)
+            )
+            if g == 0:
+                acc[chunk] = [
+                    psum.tile([P, CHUNK], F32, tag="bank", name="acc_%d" % j) for j in range(tiles)
+                ]
+            w_codes, w_scales = w_operand[u]
+            for j in range(tiles):
+                nc.tensor.matmul_mx(
+                    out=acc[chunk][j][:],
+                    lhsT=codes[:, g, j * P : (j + 1) * P].bitcast(FP8X4),
+                    lhsT_scale=code_scales[:, g, j * P : (j + 1) * P],
+                    rhs=w_codes[:].bitcast(FP8X4),
+                    rhs_scale=w_scales[:],
+                    start=(g == 0),
+                    stop=(g == PASSES - 1),
                 )
 
-            for g in range(PASSES):
-                for j in range(GROUP):
-                    for kind, first, last, slot in SPANS:
-                        lo, hi = groups_of(first, last, j)
-                        if lo < hi:
-                            s0 = slot + GROUP * lo + j - first
-                            nc.vector.tensor_copy(
-                                out=grouped_x[g][:, j, kind, SAMPLES * lo : SAMPLES * hi, :].rearrange(
-                                    "p (i b) t -> p i t b", b=SAMPLES
-                                ),
-                                in_=planes[
-                                    :, PACK * g : PACK * (g + 1), s0 : s0 + GROUP * (hi - lo - 1) + 1 : GROUP, :
-                                ].rearrange("p t i b -> p i t b"),
-                            )
-                    nc.vector.quantize_mx(
-                        out=x_codes[:, g, j, :].bitcast(FP8X4),
-                        scales=x_scales[:, g, j, :],
-                        in_=grouped_x[g][:, j].rearrange("p k c t -> p (k c t)"),
-                    )
+        result = {}
 
-        with tc.tile_pool(name="result", bufs=3) as result_pool:
-            for chunk in range(CHUNKS):
-                third, half = divmod(chunk, 2)
-                acc = [
-                    psum.tile([P, CHUNK], F32, tag="bank", name="acc_%d" % j) for j in range(GROUP)
-                ]
-                for g, kind in UNITS:
-                    source = raw[third, g, kind][:, :, half * CHUNK : (half + 1) * CHUNK]
-                    grouped_w = grouped_pool.tile([P, CHUNK, PACK], BF16, align_bytes=64)
-                    nc.vector.tensor_copy(
-                        out=grouped_w[:, 0:VECTOR_COLUMNS, :].rearrange("p (c i) t -> p c t i", i=4),
-                        in_=source[:, :, 0:VECTOR_COLUMNS].rearrange("p t (c i) -> p c t i", i=4),
-                    )
-                    nc.scalar.copy(
-                        out=grouped_w[:, VECTOR_COLUMNS:CHUNK, :].rearrange("p (c i) t -> p c t i", i=4),
-                        in_=source[:, :, VECTOR_COLUMNS:CHUNK].rearrange("p t (c i) -> p c t i", i=4),
-                    )
-                    w_codes = codes_pool.tile([P, CHUNK], U32, align_bytes=64)
-                    w_scales = codes_pool.tile([P, CHUNK], U8, align_bytes=64)
-                    nc.vector.quantize_mx(
-                        out=w_codes[:].bitcast(FP8X4),
-                        scales=w_scales[:],
-                        in_=grouped_w[:].rearrange("p c t -> p (c t)"),
-                    )
-                    for j in range(GROUP):
-                        nc.tensor.matmul_mx(
-                            out=acc[j][:],
-                            lhsT=x_codes[:, g, j, kind * P : (kind + 1) * P].bitcast(FP8X4),
-                            lhsT_scale=x_scales[:, g, j, kind * P : (kind + 1) * P],
-                            rhs=w_codes[:].bitcast(FP8X4),
-                            rhs_scale=w_scales[:],
-                            start=((g, kind) == UNITS[0]),
-                            stop=((g, kind) == UNITS[-1]),
-                        )
+        def add_bias(n, j):
+            kind, chunk = divmod(n, CHUNKS)
+            if j == 0:
+                result[n] = result_pool.tile(
+                    [P, CHUNK_HEADS, len(acc[n]), HEAD_DIM], F32, name="result_%d" % kind
+                )
+            nc.vector.tensor_tensor(
+                out=result[n][:, :, j, :],
+                in0=acc[n][j][:].rearrange("p (h d) -> p h d", d=HEAD_DIM),
+                in1=bias[kind][:, chunk * CHUNK : (chunk + 1) * CHUNK].rearrange(
+                    "p (h d) -> p h d", d=HEAD_DIM
+                ),
+                op=ALU.add,
+            )
 
-                if half == 0:
-                    spread_bias(third)
-                result = result_pool.tile([P, CHUNK_HEADS, GROUP, HEAD_DIM], F32)
-                for j in range(GROUP):
-                    nc.vector.tensor_tensor(
-                        out=result[:, :, j, :],
-                        in0=acc[j][:].rearrange("p (h d) -> p h d", d=HEAD_DIM),
-                        in1=bias[prompt_columns(j)][:, chunk * CHUNK : (chunk + 1) * CHUNK].rearrange(
-                            "p (h d) -> p h d", d=HEAD_DIM
-                        ),
-                        op=ALU.add,
-                    )
-                for b in range(SAMPLES):
+        def store(n):
+            kind, chunk = divmod(n, CHUNKS)
+            third, half = divmod(chunk, 2)
+            heads = outs[third][:, half * CHUNK_HEADS : (half + 1) * CHUNK_HEADS, :, :]
+            for b in range(SAMPLES):
+                if kind == PATCH:
                     nc.sync.dma_start(
-                        out=outs[third][
-                            b, half * CHUNK_HEADS : (half + 1) * CHUNK_HEADS, :, :
-                        ].rearrange("h (i j) d -> i h (j d)", j=GROUP),
-                        in_=result[b:P:SAMPLES, :, :, :].rearrange("p h j d -> p h (j d)"),
+                        out=heads[b, :, PROMPTS:TOKENS, :].rearrange("h (i j) d -> i h (j d)", j=TILES),
+                        in_=result[n][b:P:SAMPLES].rearrange("p h j d -> p h (j d)"),
                     )
+                else:
+                    nc.sync.dma_start(
+                        out=heads[b, :, 1 : 1 + PROMPTS, :].rearrange("h m d -> m h d"),
+                        in_=result[n][b:P:SAMPLES, :, 0, :],
+                    )
+            if kind == PATCH:
+                nc.sync.dma_start(out=heads[:, :, 0, :], in_=result[n][0:SAMPLES, :, 0, :])
+
+        nc.vector.memset(minus_half[:], -0.5)
+        nc.scalar.activation(out=scratch[:], in_=minus_half[:], func=ACT.Identity)
+        nc.scalar.dma_start(out=x_class[:], in_=x[:, 0, :])
+        load_patch(2)
+        load_piece(PATCH, 0, 0)
+        load_patch(0)
+        for g in range(PASSES):
+            if g == 1:
+                load_piece(PATCH, 0, 1)
+            load_piece(PATCH, 1, g)
+        nc.vector.memset(bias_rows[:].bitcast(F32), 0.0)
+        nc.scalar.dma_start(out=bias_rows[0:1, :], in_=b_qkv.rearrange("(o n) -> o n", o=1))
+        nc.scalar.dma_start(out=bias_rows[32:33, :], in_=b_qkv_p.rearrange("(o n) -> o n", o=1))
+        make_identity(nc, ident[:])
+        for kind in KINDS:
+            pick[kind] = keep.tile([P, P], BF16, name="pick_%d" % kind)
+            bias[kind] = keep.tile([P, OUT_WIDTH], BF16, name="bias_%d" % kind)
+            nc.gpsimd.memset(pick[kind][:].bitcast(F32), 0.0)
+            nc.gpsimd.memset(pick[kind][32 * kind : 32 * kind + 32, :], 1.0)
+        for v, vector in enumerate((n1_g, n1_b, n1p_g, n1p_b)):
+            nc.scalar.dma_start(
+                out=vectors[:, v, 0:PLANES].rearrange("p (g t) -> p g t", t=PACK),
+                in_=vector.rearrange("(g p t) -> p g t", p=P, t=PACK),
+            )
+
+        spread_bias(PATCH)
+        patch_banks = [
+            psum.tile([P, TILES, P], F32, tag="bank", name="patch_bank_%d" % r) for r in range(PLANES)
+        ]
+
+        def to_banks(a, on_scalar):
+            z = normalise(a, x_patch[:, a, :], on_scalar)
+            for r in range(PLANES):
+                nc.tensor.transpose(patch_banks[r][:, a, :], z[:, r, :], ident[:])
+
+        statistics(2, x_patch[:, 2, :])
+        statistics(3, x_patch[:, 3, :])
+        scales(2, 4)
+        to_banks(2, True)
+        to_banks(3, False)
+        interleave_unit(0)
+        nc.vector.tensor_copy(out=x_patch[0:SAMPLES, 0, :], in_=x_class[:])
+        statistics(1, x_patch[:, 1, :])
+        statistics(0, x_patch[:, 0, :])
+        scales(0, 2)
+        to_banks(1, True)
+        to_banks(0, False)
+        nc.vector.tensor_copy(out=gain_shift[:], in_=vectors[:, :, 0:PLANES])
+        interleave_unit(1)
+        quantise_unit(0)
+        interleave_unit(2)
+        quantise_unit(1)
+        for g in range(PASSES):
+            for t in range(PACK):
+                (gain_on_scalar if t < 2 else gain_on_vector)(
+                    x_planes[:, PACK * g + t, :],
+                    patch_banks[PACK * g + t][:].rearrange("p j c -> p (j c)"),
+                    0,
+                    PACK * g + t,
+                )
+            x_grouped = grouped_pool.tile([P, CHUNK, PACK], BF16, name="grouped", align_bytes=64)
+            interleave(x_grouped, x_planes[:, PACK * g : PACK * (g + 1), :], CHUNK, 256)
+            if g == 0:
+                interleave_unit(3)
+            nc.vector.quantize_mx(
+                out=x_codes[:, g, :].bitcast(FP8X4),
+                scales=x_scales[:, g, :],
+                in_=x_grouped[:].rearrange("p c t -> p (c t)"),
+            )
+        for g in range(PASSES):
+            load_piece(PATCH, 2, g)
+        for b in range(SAMPLES):
+            nc.sync.dma_start(out=x_prompt[b:P:SAMPLES, :], in_=x[b, 1 : 1 + PROMPTS, :])
+        for g in range(PASSES):
+            load_piece(PROMPT, 0, g)
+
+        for u in range(UNITS):
+            n, g = divmod(u, PASSES)
+            if u == 6:
+                statistics(TILES, x_prompt[:])
+                scales(TILES, TILES + 1)
+                z_prompt = normalise(TILES, x_prompt[:], False)
+            if u == 10:
+                prompt_banks = [
+                    psum.tile([P, PACK, P], F32, tag="bank", name="prompt_bank_%d" % h)
+                    for h in range(PASSES)
+                ]
+                for r in range(PLANES):
+                    nc.tensor.transpose(
+                        prompt_banks[r // PACK][:, r % PACK, :], z_prompt[:, r, :], ident[:]
+                    )
+                for r in range(PLANES):
+                    gain_on_scalar(p_planes[:, r, :], prompt_banks[r // PACK][:, r % PACK, :], 2, r)
+            if u == 11:
+                for h in range(PASSES):
+                    interleave(p_grouped[:, h], p_planes[:, PACK * h : PACK * (h + 1), :], P, P)
+            interleave_unit(u + 4)
+            quantise_unit(u + 2)
+            if u == CHUNKS * PASSES:
+                nc.vector.quantize_mx(
+                    out=p_codes[:].rearrange("p g c -> p (g c)").bitcast(FP8X4),
+                    scales=p_scales[:].rearrange("p g c -> p (g c)"),
+                    in_=p_grouped[:].rearrange("p g c t -> p (g c t)"),
+                )
+            multiply_unit(u)
+            if n > 0:
+                banks = len(acc[n - 1])
+                for j in range(banks * g // 2, banks * (g + 1) // 2):
+                    add_bias(n - 1, j)
+                if g == 1:
+                    store(n - 1)
+                    if n <= PASSES:
+                        load_piece(PROMPT, 1, n - 1)
+            if u == CHUNKS * PASSES:
+                spread_bias(PROMPT)
+        add_bias(2 * CHUNKS - 1, 0)
+        store(2 * CHUNKS - 1)

@@ -36,8 +36,16 @@ UNITS = 2 * CHUNKS * PASSES
 UNIT_KIND = [PATCH] * (CHUNKS * PASSES) + [PROMPT] * (CHUNKS * PASSES)
 PIECES = {PATCH: ((0, 1), (1, 2), (3, 3)), PROMPT: ((0, 3), (3, 3))}
 
-HEAD_UNITS = 4
-VECTOR_COLUMNS = [256] * HEAD_UNITS + [48] * (CHUNKS * PASSES - HEAD_UNITS) + [128] * (CHUNKS * PASSES)
+GROUPED_BUFS = 5
+QUANTISE_LEAD = 2
+HEAD_UNITS = GROUPED_BUFS + QUANTISE_LEAD
+TENSOR_UNITS = range(UNITS - 5, UNITS)
+GPSIMD_UNITS = range(PASSES + 1 + QUANTISE_LEAD + GROUPED_BUFS, UNITS - 5, PASSES)
+VECTOR_COLUMNS = [256] * HEAD_UNITS + [32] * (UNITS - HEAD_UNITS)
+GPSIMD_COLUMNS = [256 if u in GPSIMD_UNITS else 0 for u in range(UNITS)]
+RESULT_BUFS = (3, 6)
+TOKENS_ON_VECTOR = 320
+BANK_COLUMNS = 256
 
 
 def tile_block_pa_kernel(
@@ -50,16 +58,16 @@ def tile_block_pa_kernel(
     with ExitStack() as pools:
         keep = pools.enter_context(tc.tile_pool(name="keep", bufs=1))
         z_pool = pools.enter_context(tc.tile_pool(name="z", bufs=3))
-        grouped_pool = pools.enter_context(tc.tile_pool(name="grouped", bufs=5))
-        codes_pool = pools.enter_context(tc.tile_pool(name="codes", bufs=8))
+        grouped_pool = pools.enter_context(tc.tile_pool(name="grouped", bufs=GROUPED_BUFS))
+        codes_pool = pools.enter_context(tc.tile_pool(name="codes", bufs=6))
         result_pool = pools.enter_context(tc.tile_pool(name="result", bufs=3))
         psum = pools.enter_context(tc.psum_pool(name="psum", bufs=8))
         pools.enter_context(tc.manual_schedule())
 
         minus_half = keep.tile([P, 2], F32)
         scratch = keep.tile([P, 2], F32)
-        bias_rows = keep.tile([P, OUT_WIDTH], BF16)
         ident = keep.tile([P, P], F32)
+        ident_bf16 = keep.tile([P, P], BF16)
         x_class = keep.tile([SAMPLES, WIDTH], BF16)
         vectors = keep.tile([P, 4, 2 * PLANES], BF16)
         gain_shift = keep.tile([P, 4, PLANES], F32)
@@ -102,46 +110,34 @@ def tile_block_pa_kernel(
             for c in range(chunks):
                 raw[kind, first + c, g] = piece[:, :, c * CHUNK : (c + 1) * CHUNK]
 
-        pick = {}
-        bias = {}
+        bias = {
+            kind: keep.tile([P, OUT_WIDTH], BF16, name="bias_%d" % kind) for kind in KINDS
+        }
 
-        def spread_bias(kind):
-            for third in range(3):
-                bank = psum.tile([P, TENSOR_WIDTH], BF16, tag="bank", name="bias_bank")
-                for half in range(2):
-                    first = third * TENSOR_WIDTH + half * CHUNK
-                    nc.tensor.matmul(
-                        out=bank[:, half * CHUNK : (half + 1) * CHUNK],
-                        lhsT=pick[kind][:],
-                        rhs=bias_rows[:, first : first + CHUNK],
-                        start=True,
-                        stop=True,
-                    )
-                nc.scalar.copy(
-                    out=bias[kind][:, third * TENSOR_WIDTH : (third + 1) * TENSOR_WIDTH], in_=bank[:]
-                )
+        def load_bias(kind):
+            nc.sync.dma_start(
+                out=bias[kind][:], in_=(b_qkv, b_qkv_p)[kind].partition_broadcast(P)
+            )
 
-        def statistics(a, rows):
-            for half in range(2):
-                nc.vector.bn_stats(
-                    out=stats[:, a, half, :], in_=rows[:, half * K_PASS : (half + 1) * K_PASS]
-                )
+        def half_statistics(a, rows, half):
+            nc.vector.bn_stats(
+                out=stats[:, a, half, :], in_=rows[:, half * K_PASS : (half + 1) * K_PASS]
+            )
+
+        def join_statistics(a):
             nc.vector.bn_aggr(
                 out=mean_var[:, a, :], in_=stats[:, a, :, :].rearrange("p h s -> p (h s)")
             )
 
-        def scales(lo, hi):
-            nc.vector.tensor_scalar_add(
-                out=var_eps[:, lo:hi], in0=mean_var[:, lo:hi, 1], scalar1=EPS
-            )
-            nc.vector.tensor_scalar_mul(
-                out=minus_mean[:, lo:hi], in0=mean_var[:, lo:hi, 0], scalar1=-1.0
+        def scales(a):
+            col = slice(a, a + 1)
+            nc.vector.tensor_scalar_add(out=var_eps[:, col], in0=mean_var[:, a, 1:2], scalar1=EPS)
+            nc.vector.tensor_scalar_mul(out=minus_mean[:, col], in0=mean_var[:, a, 0:1], scalar1=-1.0)
+            nc.gpsimd.tensor_tensor(
+                out=rstd[:, col], in0=var_eps[:, col], in1=minus_half[:, 0:1], op=ALU.pow
             )
             nc.gpsimd.tensor_tensor(
-                out=rstd[:, lo:hi], in0=var_eps[:, lo:hi], in1=minus_half[:, 0 : hi - lo], op=ALU.pow
-            )
-            nc.gpsimd.tensor_tensor(
-                out=minus_mean_rstd[:, lo:hi], in0=minus_mean[:, lo:hi], in1=rstd[:, lo:hi], op=ALU.mult
+                out=minus_mean_rstd[:, col], in0=minus_mean[:, col], in1=rstd[:, col], op=ALU.mult
             )
 
         def normalise(a, rows, on_scalar):
@@ -186,27 +182,62 @@ def tile_block_pa_kernel(
                 op1=ALU.add,
             )
 
-        def interleave(dst, src, columns, vector_columns):
-            for copy, lo, hi in (
-                (nc.scalar.copy, vector_columns, columns),
-                (nc.vector.tensor_copy, 0, vector_columns),
-            ):
-                if lo < hi:
-                    copy(
-                        out=dst[:, lo:hi, :].rearrange("p (c i) t -> p c t i", i=4),
-                        in_=src[:, :, lo:hi].rearrange("p t (c i) -> p c t i", i=4),
-                    )
+        def interleave_on_vector(dst, src, lo, hi):
+            nc.vector.tensor_copy(
+                out=dst[:, lo:hi, :].rearrange("p (c i) t -> p c t i", i=4),
+                in_=src[:, :, lo:hi].rearrange("p t (c i) -> p c t i", i=4),
+            )
+
+        def interleave_on_scalar(dst, src, lo, hi):
+            nc.scalar.copy(
+                out=dst[:, lo:hi, :].rearrange("p (c i) t -> p c t i", i=4),
+                in_=src[:, :, lo:hi].rearrange("p t (c i) -> p c t i", i=4),
+            )
+
+        def interleave_on_gpsimd(dst, src, lo, hi):
+            nc.gpsimd.tensor_scalar(
+                out=dst[:, lo:hi, :],
+                in0=src[:, :, lo:hi].rearrange("p t c -> p c t"),
+                scalar1=1.0,
+                scalar2=0.0,
+                op0=ALU.mult,
+                op1=ALU.add,
+            )
 
         grouped = {}
         w_operand = {}
 
-        def interleave_unit(u):
+        def weight(u):
+            chunk, g = divmod(u % (CHUNKS * PASSES), PASSES)
+            return raw[UNIT_KIND[u], chunk, g]
+
+        def unit_on_scalar(u):
             if u < UNITS:
-                chunk, g = divmod(u % (CHUNKS * PASSES), PASSES)
                 grouped[u] = grouped_pool.tile(
                     [P, CHUNK, PACK], BF16, name="grouped", align_bytes=64
                 )
-                interleave(grouped[u], raw[UNIT_KIND[u], chunk, g], CHUNK, VECTOR_COLUMNS[u])
+                if u in TENSOR_UNITS:
+                    for lo in range(0, CHUNK, BANK_COLUMNS):
+                        bank = psum.tile([P, BANK_COLUMNS, PACK], BF16, tag="bank", name="group_bank")
+                        for c in range(0, BANK_COLUMNS, P):
+                            nc.tensor.matmul(
+                                out=bank[:, c : c + P, :].rearrange("p c t -> p t c"),
+                                lhsT=ident_bf16[:],
+                                rhs=weight(u)[:, :, lo + c : lo + c + P],
+                                start=True,
+                                stop=True,
+                            )
+                        nc.scalar.copy(out=grouped[u][:, lo : lo + BANK_COLUMNS, :], in_=bank[:])
+                    return
+                lo = VECTOR_COLUMNS[u]
+                hi = lo + GPSIMD_COLUMNS[u]
+                if hi > lo:
+                    interleave_on_gpsimd(grouped[u], weight(u), lo, hi)
+                interleave_on_scalar(grouped[u], weight(u), hi, CHUNK)
+
+        def unit_on_vector(u):
+            if u < UNITS and u not in TENSOR_UNITS:
+                interleave_on_vector(grouped[u], weight(u), 0, VECTOR_COLUMNS[u])
 
         def quantise_unit(u):
             if u < UNITS:
@@ -249,7 +280,10 @@ def tile_block_pa_kernel(
             kind, chunk = divmod(n, CHUNKS)
             if j == 0:
                 result[n] = result_pool.tile(
-                    [P, CHUNK_HEADS, len(acc[n]), HEAD_DIM], F32, name="result_%d" % kind
+                    [P, CHUNK_HEADS, len(acc[n]), HEAD_DIM],
+                    F32,
+                    name="result_%d" % kind,
+                    bufs=RESULT_BUFS[kind],
                 )
             nc.vector.tensor_tensor(
                 out=result[n][:, :, j, :],
@@ -284,114 +318,126 @@ def tile_block_pa_kernel(
         load_patch(2)
         load_piece(PATCH, 0, 0)
         load_patch(0)
-        for g in range(PASSES):
-            if g == 1:
-                load_piece(PATCH, 0, 1)
-            load_piece(PATCH, 1, g)
-        nc.vector.memset(bias_rows[:].bitcast(F32), 0.0)
-        nc.scalar.dma_start(out=bias_rows[0:1, :], in_=b_qkv.rearrange("(o n) -> o n", o=1))
-        nc.scalar.dma_start(out=bias_rows[32:33, :], in_=b_qkv_p.rearrange("(o n) -> o n", o=1))
+        load_piece(PATCH, 0, 1)
+        load_piece(PATCH, 1, 0)
+        for b in range(SAMPLES):
+            nc.sync.dma_start(out=x_prompt[b:P:SAMPLES, :], in_=x[b, 1 : 1 + PROMPTS, :])
+        load_piece(PATCH, 1, 1)
         make_identity(nc, ident[:])
-        for kind in KINDS:
-            pick[kind] = keep.tile([P, P], BF16, name="pick_%d" % kind)
-            bias[kind] = keep.tile([P, OUT_WIDTH], BF16, name="bias_%d" % kind)
-            nc.gpsimd.memset(pick[kind][:].bitcast(F32), 0.0)
-            nc.gpsimd.memset(pick[kind][32 * kind : 32 * kind + 32, :], 1.0)
+        make_identity(nc, ident_bf16[:])
         for v, vector in enumerate((n1_g, n1_b, n1p_g, n1p_b)):
             nc.scalar.dma_start(
                 out=vectors[:, v, 0:PLANES].rearrange("p (g t) -> p g t", t=PACK),
                 in_=vector.rearrange("(g p t) -> p g t", p=P, t=PACK),
             )
 
-        spread_bias(PATCH)
         patch_banks = [
             psum.tile([P, TILES, P], F32, tag="bank", name="patch_bank_%d" % r) for r in range(PLANES)
         ]
 
-        def to_banks(a, on_scalar):
-            z = normalise(a, x_patch[:, a, :], on_scalar)
+        def patch_to_banks(a):
+            z = normalise(a, x_patch[:, a, :], True)
             for r in range(PLANES):
                 nc.tensor.transpose(patch_banks[r][:, a, :], z[:, r, :], ident[:])
 
-        statistics(2, x_patch[:, 2, :])
-        statistics(3, x_patch[:, 3, :])
-        scales(2, 4)
-        to_banks(2, True)
-        to_banks(3, False)
-        interleave_unit(0)
+        unit_on_scalar(0)
+        half_statistics(2, x_patch[:, 2, :], 0)
+        half_statistics(2, x_patch[:, 2, :], 1)
+        half_statistics(3, x_patch[:, 3, :], 0)
+        join_statistics(2)
+        half_statistics(3, x_patch[:, 3, :], 1)
+        scales(2)
+        patch_to_banks(2)
+        unit_on_vector(0)
+        join_statistics(3)
         nc.vector.tensor_copy(out=x_patch[0:SAMPLES, 0, :], in_=x_class[:])
-        statistics(1, x_patch[:, 1, :])
-        statistics(0, x_patch[:, 0, :])
-        scales(0, 2)
-        to_banks(1, True)
-        to_banks(0, False)
-        nc.vector.tensor_copy(out=gain_shift[:], in_=vectors[:, :, 0:PLANES])
-        interleave_unit(1)
+        scales(3)
+        patch_to_banks(3)
+        half_statistics(1, x_patch[:, 1, :], 0)
+        half_statistics(1, x_patch[:, 1, :], 1)
+        half_statistics(0, x_patch[:, 0, :], 0)
+        join_statistics(1)
+        half_statistics(0, x_patch[:, 0, :], 1)
+        scales(1)
+        unit_on_scalar(1)
+        patch_to_banks(1)
         quantise_unit(0)
-        interleave_unit(2)
+        join_statistics(0)
+        unit_on_vector(1)
+        scales(0)
+        patch_to_banks(0)
+        nc.vector.tensor_copy(out=gain_shift[:], in_=vectors[:, :, 0:PLANES])
+        unit_on_scalar(2)
+        half_statistics(TILES, x_prompt[:], 0)
+        half_statistics(TILES, x_prompt[:], 1)
+        unit_on_vector(2)
+        join_statistics(TILES)
         quantise_unit(1)
+        scales(TILES)
+        z_prompt = normalise(TILES, x_prompt[:], False)
+        x_grouped = [
+            keep.tile([P, CHUNK, PACK], BF16, name="x_grouped_%d" % g, align_bytes=64)
+            for g in range(PASSES)
+        ]
+        for r in range(PLANES):
+            (gain_on_scalar if r % PACK < 2 else gain_on_vector)(
+                x_planes[:, r, :], patch_banks[r][:].rearrange("p j c -> p (j c)"), 0, r
+            )
         for g in range(PASSES):
-            for t in range(PACK):
-                (gain_on_scalar if t < 2 else gain_on_vector)(
-                    x_planes[:, PACK * g + t, :],
-                    patch_banks[PACK * g + t][:].rearrange("p j c -> p (j c)"),
-                    0,
-                    PACK * g + t,
-                )
-            x_grouped = grouped_pool.tile([P, CHUNK, PACK], BF16, name="grouped", align_bytes=64)
-            interleave(x_grouped, x_planes[:, PACK * g : PACK * (g + 1), :], CHUNK, 256)
-            if g == 0:
-                interleave_unit(3)
+            planes = x_planes[:, PACK * g : PACK * (g + 1), :]
+            interleave_on_scalar(x_grouped[g], planes, TOKENS_ON_VECTOR, CHUNK)
+            interleave_on_vector(x_grouped[g], planes, 0, TOKENS_ON_VECTOR)
+        for g in range(PASSES):
             nc.vector.quantize_mx(
                 out=x_codes[:, g, :].bitcast(FP8X4),
                 scales=x_scales[:, g, :],
-                in_=x_grouped[:].rearrange("p c t -> p (c t)"),
+                in_=x_grouped[g][:].rearrange("p c t -> p (c t)"),
             )
+        prompt_banks = [
+            psum.tile([P, PACK, P], F32, tag="bank", name="prompt_bank_%d" % g) for g in range(PASSES)
+        ]
+        for r in range(PLANES):
+            nc.tensor.transpose(prompt_banks[r // PACK][:, r % PACK, :], z_prompt[:, r, :], ident[:])
+        unit_on_scalar(3)
+        for r in range(PLANES):
+            gain_on_scalar(p_planes[:, r, :], prompt_banks[r // PACK][:, r % PACK, :], 2, r)
+        unit_on_scalar(4)
+        unit_on_vector(3)
+        unit_on_vector(4)
         for g in range(PASSES):
             load_piece(PATCH, 2, g)
-        for b in range(SAMPLES):
-            nc.sync.dma_start(out=x_prompt[b:P:SAMPLES, :], in_=x[b, 1 : 1 + PROMPTS, :])
+        load_bias(PATCH)
+        for u in range(GROUPED_BUFS, GROUPED_BUFS + QUANTISE_LEAD):
+            unit_on_scalar(u)
+        unit_on_vector(GROUPED_BUFS)
         for g in range(PASSES):
             load_piece(PROMPT, 0, g)
 
         for u in range(UNITS):
             n, g = divmod(u, PASSES)
-            if u == 6:
-                statistics(TILES, x_prompt[:])
-                scales(TILES, TILES + 1)
-                z_prompt = normalise(TILES, x_prompt[:], False)
-            if u == 10:
-                prompt_banks = [
-                    psum.tile([P, PACK, P], F32, tag="bank", name="prompt_bank_%d" % h)
-                    for h in range(PASSES)
-                ]
-                for r in range(PLANES):
-                    nc.tensor.transpose(
-                        prompt_banks[r // PACK][:, r % PACK, :], z_prompt[:, r, :], ident[:]
-                    )
-                for r in range(PLANES):
-                    gain_on_scalar(p_planes[:, r, :], prompt_banks[r // PACK][:, r % PACK, :], 2, r)
-            if u == 11:
+            ahead = u + QUANTISE_LEAD + GROUPED_BUFS
+            quantise_unit(u + QUANTISE_LEAD)
+            unit_on_scalar(ahead)
+            multiply_unit(u)
+            if n > 0 and g == 1:
+                for j in range(len(acc[n - 1])):
+                    add_bias(n - 1, j)
+                store(n - 1)
+                if n <= PASSES:
+                    load_piece(PROMPT, 1, n - 1)
+                if n == PASSES:
+                    load_bias(PROMPT)
+            unit_on_vector(ahead - 1)
+            if u == 1:
                 for h in range(PASSES):
-                    interleave(p_grouped[:, h], p_planes[:, PACK * h : PACK * (h + 1), :], P, P)
-            interleave_unit(u + 4)
-            quantise_unit(u + 2)
-            if u == CHUNKS * PASSES:
+                    interleave_on_vector(
+                        p_grouped[:, h], p_planes[:, PACK * h : PACK * (h + 1), :], 0, P
+                    )
+            if u == 2:
                 nc.vector.quantize_mx(
                     out=p_codes[:].rearrange("p g c -> p (g c)").bitcast(FP8X4),
                     scales=p_scales[:].rearrange("p g c -> p (g c)"),
                     in_=p_grouped[:].rearrange("p g c t -> p (g c t)"),
                 )
-            multiply_unit(u)
-            if n > 0:
-                banks = len(acc[n - 1])
-                for j in range(banks * g // 2, banks * (g + 1) // 2):
-                    add_bias(n - 1, j)
-                if g == 1:
-                    store(n - 1)
-                    if n <= PASSES:
-                        load_piece(PROMPT, 1, n - 1)
-            if u == CHUNKS * PASSES:
-                spread_bias(PROMPT)
         add_bias(2 * CHUNKS - 1, 0)
         store(2 * CHUNKS - 1)

@@ -36,15 +36,18 @@ UNITS = 2 * CHUNKS * PASSES
 UNIT_KIND = [PATCH] * (CHUNKS * PASSES) + [PROMPT] * (CHUNKS * PASSES)
 PIECES = {PATCH: ((0, 1), (1, 2), (3, 3)), PROMPT: ((0, 3), (3, 3))}
 
+LATE_UNIT = 18
 GROUPED_BUFS = 5
 QUANTISE_LEAD = 2
 HEAD_UNITS = GROUPED_BUFS + QUANTISE_LEAD
-TENSOR_UNITS = range(UNITS - 5, UNITS)
-GPSIMD_UNITS = range(PASSES + 1 + QUANTISE_LEAD + GROUPED_BUFS, UNITS - 5, PASSES)
-VECTOR_COLUMNS = [256] * HEAD_UNITS + [32] * (UNITS - HEAD_UNITS)
-GPSIMD_COLUMNS = [256 if u in GPSIMD_UNITS else 0 for u in range(UNITS)]
-RESULT_BUFS = (3, 6)
-TOKENS_ON_VECTOR = 320
+TENSOR_UNITS = (UNITS - 2, UNITS - 1)
+GPSIMD_UNITS = range(PASSES + 1 + HEAD_UNITS, LATE_UNIT + 2, PASSES)
+TENSOR_COLUMNS = [CHUNK if u in TENSOR_UNITS else 0 for u in range(UNITS)]
+GPSIMD_COLUMNS = [320 if u in GPSIMD_UNITS else 0 for u in range(UNITS)]
+VECTOR_COLUMNS = [256] * HEAD_UNITS + [16] * (LATE_UNIT - HEAD_UNITS) + [192] * 4 + [0] * 2
+BIAS_TURNS = (11, 12, 13)
+RESULT_BUFS = (5, 6)
+TOKENS_ON_VECTOR = 384
 BANK_COLUMNS = 256
 
 
@@ -57,10 +60,8 @@ def tile_block_pa_kernel(
 
     with ExitStack() as pools:
         keep = pools.enter_context(tc.tile_pool(name="keep", bufs=1))
-        z_pool = pools.enter_context(tc.tile_pool(name="z", bufs=3))
         grouped_pool = pools.enter_context(tc.tile_pool(name="grouped", bufs=GROUPED_BUFS))
         codes_pool = pools.enter_context(tc.tile_pool(name="codes", bufs=6))
-        result_pool = pools.enter_context(tc.tile_pool(name="result", bufs=3))
         psum = pools.enter_context(tc.psum_pool(name="psum", bufs=8))
         pools.enter_context(tc.manual_schedule())
 
@@ -69,9 +70,10 @@ def tile_block_pa_kernel(
         ident = keep.tile([P, P], F32)
         ident_bf16 = keep.tile([P, P], BF16)
         x_class = keep.tile([SAMPLES, WIDTH], BF16)
+        bias_rows = keep.tile([P, OUT_WIDTH], BF16)
+        pick = {kind: keep.tile([P, P], BF16, name="pick_%d" % kind) for kind in KINDS}
         vectors = keep.tile([P, 4, 2 * PLANES], BF16)
         gain_shift = keep.tile([P, 4, PLANES], F32)
-        x_patch = keep.tile([P, TILES, WIDTH], BF16)
         x_prompt = keep.tile([P, WIDTH], BF16)
         stats = keep.tile([P, TILES + 1, 2, 6], F32)
         mean_var = keep.tile([P, TILES + 1, 2], F32)
@@ -79,7 +81,6 @@ def tile_block_pa_kernel(
         rstd = keep.tile([P, TILES + 1], F32)
         minus_mean = keep.tile([P, TILES + 1], F32)
         minus_mean_rstd = keep.tile([P, TILES + 1], F32)
-        x_planes = keep.tile([P, PLANES, TILES * P], BF16)
         x_codes = keep.tile([P, PASSES, TILES * P], U32, align_bytes=64)
         x_scales = keep.tile([P, PASSES, TILES * P], U8, align_bytes=64)
         p_planes = keep.tile([P, PLANES, P], BF16)
@@ -87,7 +88,7 @@ def tile_block_pa_kernel(
         p_codes = keep.tile([P, PASSES, P], U32, align_bytes=64)
         p_scales = keep.tile([P, PASSES, P], U8, align_bytes=64)
 
-        def load_patch(j):
+        def load_patch(x_patch, j):
             for b in range(SAMPLES):
                 nc.sync.dma_start(
                     out=x_patch[b:P:SAMPLES, j : j + 2, :],
@@ -114,9 +115,19 @@ def tile_block_pa_kernel(
             kind: keep.tile([P, OUT_WIDTH], BF16, name="bias_%d" % kind) for kind in KINDS
         }
 
-        def load_bias(kind):
-            nc.sync.dma_start(
-                out=bias[kind][:], in_=(b_qkv, b_qkv_p)[kind].partition_broadcast(P)
+        def spread_bias(kind, third):
+            bank = psum.tile([P, TENSOR_WIDTH], BF16, tag="bank", name="bias_bank")
+            for half in range(2):
+                first = third * TENSOR_WIDTH + half * CHUNK
+                nc.tensor.matmul(
+                    out=bank[:, half * CHUNK : (half + 1) * CHUNK],
+                    lhsT=pick[kind][:],
+                    rhs=bias_rows[:, first : first + CHUNK],
+                    start=True,
+                    stop=True,
+                )
+            nc.scalar.copy(
+                out=bias[kind][:, third * TENSOR_WIDTH : (third + 1) * TENSOR_WIDTH], in_=bank[:]
             )
 
         def half_statistics(a, rows, half):
@@ -140,8 +151,7 @@ def tile_block_pa_kernel(
                 out=minus_mean_rstd[:, col], in0=minus_mean[:, col], in1=rstd[:, col], op=ALU.mult
             )
 
-        def normalise(a, rows, on_scalar):
-            z = z_pool.tile([P, PLANES, P], F32, name="z")
+        def normalise(z, a, rows, on_scalar):
             out = z[:].rearrange("q (g t) p -> q g t p", t=PACK)
             in_ = rows.rearrange("q (g p t) -> q g t p", p=P, t=PACK)
             if on_scalar:
@@ -161,7 +171,6 @@ def tile_block_pa_kernel(
                     op0=ALU.mult,
                     op1=ALU.add,
                 )
-            return z
 
         def gain_on_scalar(out, bank, vector, r):
             nc.scalar.activation(
@@ -216,27 +225,27 @@ def tile_block_pa_kernel(
                 grouped[u] = grouped_pool.tile(
                     [P, CHUNK, PACK], BF16, name="grouped", align_bytes=64
                 )
-                if u in TENSOR_UNITS:
-                    for lo in range(0, CHUNK, BANK_COLUMNS):
-                        bank = psum.tile([P, BANK_COLUMNS, PACK], BF16, tag="bank", name="group_bank")
-                        for c in range(0, BANK_COLUMNS, P):
-                            nc.tensor.matmul(
-                                out=bank[:, c : c + P, :].rearrange("p c t -> p t c"),
-                                lhsT=ident_bf16[:],
-                                rhs=weight(u)[:, :, lo + c : lo + c + P],
-                                start=True,
-                                stop=True,
-                            )
-                        nc.scalar.copy(out=grouped[u][:, lo : lo + BANK_COLUMNS, :], in_=bank[:])
-                    return
                 lo = VECTOR_COLUMNS[u]
                 hi = lo + GPSIMD_COLUMNS[u]
+                end = CHUNK - TENSOR_COLUMNS[u]
                 if hi > lo:
                     interleave_on_gpsimd(grouped[u], weight(u), lo, hi)
-                interleave_on_scalar(grouped[u], weight(u), hi, CHUNK)
+                for first in range(end, CHUNK, BANK_COLUMNS):
+                    bank = psum.tile([P, BANK_COLUMNS, PACK], BF16, tag="bank", name="group_bank")
+                    for c in range(0, BANK_COLUMNS, P):
+                        nc.tensor.matmul(
+                            out=bank[:, c : c + P, :].rearrange("p c t -> p t c"),
+                            lhsT=ident_bf16[:],
+                            rhs=weight(u)[:, :, first + c : first + c + P],
+                            start=True,
+                            stop=True,
+                        )
+                    nc.scalar.copy(out=grouped[u][:, first : first + BANK_COLUMNS, :], in_=bank[:])
+                if end > hi:
+                    interleave_on_scalar(grouped[u], weight(u), hi, end)
 
         def unit_on_vector(u):
-            if u < UNITS and u not in TENSOR_UNITS:
+            if u < UNITS and VECTOR_COLUMNS[u] > 0:
                 interleave_on_vector(grouped[u], weight(u), 0, VECTOR_COLUMNS[u])
 
         def quantise_unit(u):
@@ -312,92 +321,114 @@ def tile_block_pa_kernel(
             if kind == PATCH:
                 nc.sync.dma_start(out=heads[:, :, 0, :], in_=result[n][0:SAMPLES, :, 0, :])
 
-        nc.vector.memset(minus_half[:], -0.5)
-        nc.scalar.activation(out=scratch[:], in_=minus_half[:], func=ACT.Identity)
-        nc.scalar.dma_start(out=x_class[:], in_=x[:, 0, :])
-        load_patch(2)
-        load_piece(PATCH, 0, 0)
-        load_patch(0)
-        load_piece(PATCH, 0, 1)
-        load_piece(PATCH, 1, 0)
-        for b in range(SAMPLES):
-            nc.sync.dma_start(out=x_prompt[b:P:SAMPLES, :], in_=x[b, 1 : 1 + PROMPTS, :])
-        load_piece(PATCH, 1, 1)
-        make_identity(nc, ident[:])
-        make_identity(nc, ident_bf16[:])
-        for v, vector in enumerate((n1_g, n1_b, n1p_g, n1p_b)):
-            nc.scalar.dma_start(
-                out=vectors[:, v, 0:PLANES].rearrange("p (g t) -> p g t", t=PACK),
-                in_=vector.rearrange("(g p t) -> p g t", p=P, t=PACK),
-            )
+        with tc.tile_pool(name="head", bufs=1) as head, tc.tile_pool(name="z", bufs=3) as z_pool:
+            x_patch = head.tile([P, TILES, WIDTH], BF16)
+            x_planes = head.tile([P, PLANES, TILES * P], BF16)
+            x_grouped = [
+                head.tile([P, CHUNK, PACK], BF16, name="x_grouped_%d" % g, align_bytes=64)
+                for g in range(PASSES)
+            ]
+            nc.vector.memset(minus_half[:], -0.5)
+            half_row = TENSOR_WIDTH + CHUNK
+            nc.vector.memset(bias_rows[:, 0:half_row].bitcast(F32), 0.0)
+            nc.gpsimd.memset(bias_rows[:, half_row:OUT_WIDTH].bitcast(F32), 0.0)
+            nc.scalar.activation(out=scratch[:], in_=minus_half[:], func=ACT.Identity)
+            nc.gpsimd.dma_start(out=bias_rows[0:1, :], in_=b_qkv.rearrange("(o n) -> o n", o=1))
+            nc.gpsimd.dma_start(out=bias_rows[32:33, :], in_=b_qkv_p.rearrange("(o n) -> o n", o=1))
+            nc.gpsimd.dma_start(out=x_class[:], in_=x[:, 0, :])
+            load_patch(x_patch, 2)
+            load_piece(PATCH, 0, 0)
+            load_patch(x_patch, 0)
+            load_piece(PATCH, 0, 1)
+            load_piece(PATCH, 1, 0)
+            for b in range(SAMPLES):
+                nc.sync.dma_start(out=x_prompt[b:P:SAMPLES, :], in_=x[b, 1 : 1 + PROMPTS, :])
+            load_piece(PATCH, 1, 1)
+            for g in range(PASSES):
+                load_piece(PATCH, 2, g)
+            for kind in KINDS:
+                nc.gpsimd.memset(pick[kind][:].bitcast(F32), 0.0)
+                nc.gpsimd.memset(pick[kind][32 * kind : 32 * kind + 32, :], 1.0)
+            make_identity(nc, ident[:])
+            make_identity(nc, ident_bf16[:])
+            for v, vector in enumerate((n1_g, n1_b, n1p_g, n1p_b)):
+                nc.scalar.dma_start(
+                    out=vectors[:, v, 0:PLANES].rearrange("p (g t) -> p g t", t=PACK),
+                    in_=vector.rearrange("(g p t) -> p g t", p=P, t=PACK),
+                )
 
-        patch_banks = [
-            psum.tile([P, TILES, P], F32, tag="bank", name="patch_bank_%d" % r) for r in range(PLANES)
-        ]
+            unit_on_scalar(0)
+            for third in range(3):
+                spread_bias(PATCH, third)
+            patch_banks = [
+                psum.tile([P, TILES, P], F32, tag="bank", name="patch_bank_%d" % r)
+                for r in range(PLANES)
+            ]
 
-        def patch_to_banks(a):
-            z = normalise(a, x_patch[:, a, :], True)
+            def patch_to_banks(a):
+                z = z_pool.tile([P, PLANES, P], F32, name="z")
+                normalise(z, a, x_patch[:, a, :], True)
+                for r in range(PLANES):
+                    nc.tensor.transpose(patch_banks[r][:, a, :], z[:, r, :], ident[:])
+
+            half_statistics(2, x_patch[:, 2, :], 0)
+            half_statistics(2, x_patch[:, 2, :], 1)
+            half_statistics(3, x_patch[:, 3, :], 0)
+            join_statistics(2)
+            half_statistics(3, x_patch[:, 3, :], 1)
+            scales(2)
+            patch_to_banks(2)
+            half_statistics(1, x_patch[:, 1, :], 0)
+            join_statistics(3)
+            nc.vector.tensor_copy(out=x_patch[0:SAMPLES, 0, :], in_=x_class[:])
+            scales(3)
+            patch_to_banks(3)
+            half_statistics(1, x_patch[:, 1, :], 1)
+            half_statistics(0, x_patch[:, 0, :], 0)
+            join_statistics(1)
+            half_statistics(0, x_patch[:, 0, :], 1)
+            scales(1)
+            patch_to_banks(1)
+            unit_on_vector(0)
+            join_statistics(0)
+            unit_on_scalar(1)
+            unit_on_vector(1)
+            scales(0)
+            quantise_unit(0)
+            patch_to_banks(0)
+            nc.vector.tensor_copy(out=gain_shift[:], in_=vectors[:, :, 0:PLANES])
+            unit_on_scalar(2)
+            half_statistics(TILES, x_prompt[:], 0)
+            half_statistics(TILES, x_prompt[:], 1)
+            unit_on_vector(2)
+            join_statistics(TILES)
+            quantise_unit(1)
+            scales(TILES)
+            z_prompt = z_pool.tile([P, PLANES, P], F32, name="z")
+            normalise(z_prompt, TILES, x_prompt[:], False)
             for r in range(PLANES):
-                nc.tensor.transpose(patch_banks[r][:, a, :], z[:, r, :], ident[:])
-
-        unit_on_scalar(0)
-        half_statistics(2, x_patch[:, 2, :], 0)
-        half_statistics(2, x_patch[:, 2, :], 1)
-        half_statistics(3, x_patch[:, 3, :], 0)
-        join_statistics(2)
-        half_statistics(3, x_patch[:, 3, :], 1)
-        scales(2)
-        patch_to_banks(2)
-        unit_on_vector(0)
-        join_statistics(3)
-        nc.vector.tensor_copy(out=x_patch[0:SAMPLES, 0, :], in_=x_class[:])
-        scales(3)
-        patch_to_banks(3)
-        half_statistics(1, x_patch[:, 1, :], 0)
-        half_statistics(1, x_patch[:, 1, :], 1)
-        half_statistics(0, x_patch[:, 0, :], 0)
-        join_statistics(1)
-        half_statistics(0, x_patch[:, 0, :], 1)
-        scales(1)
-        unit_on_scalar(1)
-        patch_to_banks(1)
-        quantise_unit(0)
-        join_statistics(0)
-        unit_on_vector(1)
-        scales(0)
-        patch_to_banks(0)
-        nc.vector.tensor_copy(out=gain_shift[:], in_=vectors[:, :, 0:PLANES])
-        unit_on_scalar(2)
-        half_statistics(TILES, x_prompt[:], 0)
-        half_statistics(TILES, x_prompt[:], 1)
-        unit_on_vector(2)
-        join_statistics(TILES)
-        quantise_unit(1)
-        scales(TILES)
-        z_prompt = normalise(TILES, x_prompt[:], False)
-        x_grouped = [
-            keep.tile([P, CHUNK, PACK], BF16, name="x_grouped_%d" % g, align_bytes=64)
-            for g in range(PASSES)
-        ]
-        for r in range(PLANES):
-            (gain_on_scalar if r % PACK < 2 else gain_on_vector)(
-                x_planes[:, r, :], patch_banks[r][:].rearrange("p j c -> p (j c)"), 0, r
-            )
-        for g in range(PASSES):
-            planes = x_planes[:, PACK * g : PACK * (g + 1), :]
-            interleave_on_scalar(x_grouped[g], planes, TOKENS_ON_VECTOR, CHUNK)
-            interleave_on_vector(x_grouped[g], planes, 0, TOKENS_ON_VECTOR)
-        for g in range(PASSES):
-            nc.vector.quantize_mx(
-                out=x_codes[:, g, :].bitcast(FP8X4),
-                scales=x_scales[:, g, :],
-                in_=x_grouped[g][:].rearrange("p c t -> p (c t)"),
-            )
-        prompt_banks = [
-            psum.tile([P, PACK, P], F32, tag="bank", name="prompt_bank_%d" % g) for g in range(PASSES)
-        ]
-        for r in range(PLANES):
-            nc.tensor.transpose(prompt_banks[r // PACK][:, r % PACK, :], z_prompt[:, r, :], ident[:])
+                (gain_on_scalar if r % PACK < 2 else gain_on_vector)(
+                    x_planes[:, r, :], patch_banks[r][:].rearrange("p j c -> p (j c)"), 0, r
+                )
+            for g in range(PASSES):
+                planes = x_planes[:, PACK * g : PACK * (g + 1), :]
+                interleave_on_scalar(x_grouped[g], planes, TOKENS_ON_VECTOR, CHUNK)
+                interleave_on_vector(x_grouped[g], planes, 0, TOKENS_ON_VECTOR)
+            for g in range(PASSES):
+                nc.vector.quantize_mx(
+                    out=x_codes[:, g, :].bitcast(FP8X4),
+                    scales=x_scales[:, g, :],
+                    in_=x_grouped[g][:].rearrange("p c t -> p (c t)"),
+                )
+            prompt_banks = [
+                psum.tile([P, PACK, P], F32, tag="bank", name="prompt_bank_%d" % g)
+                for g in range(PASSES)
+            ]
+            for r in range(PLANES):
+                nc.tensor.transpose(
+                    prompt_banks[r // PACK][:, r % PACK, :], z_prompt[:, r, :], ident[:]
+                )
+        result_pool = pools.enter_context(tc.tile_pool(name="result", bufs=1))
         unit_on_scalar(3)
         for r in range(PLANES):
             gain_on_scalar(p_planes[:, r, :], prompt_banks[r // PACK][:, r % PACK, :], 2, r)
@@ -405,13 +436,11 @@ def tile_block_pa_kernel(
         unit_on_vector(3)
         unit_on_vector(4)
         for g in range(PASSES):
-            load_piece(PATCH, 2, g)
-        load_bias(PATCH)
+            load_piece(PROMPT, 0, g)
+        load_piece(PROMPT, 1, 0)
         for u in range(GROUPED_BUFS, GROUPED_BUFS + QUANTISE_LEAD):
             unit_on_scalar(u)
         unit_on_vector(GROUPED_BUFS)
-        for g in range(PASSES):
-            load_piece(PROMPT, 0, g)
 
         for u in range(UNITS):
             n, g = divmod(u, PASSES)
@@ -423,11 +452,11 @@ def tile_block_pa_kernel(
                 for j in range(len(acc[n - 1])):
                     add_bias(n - 1, j)
                 store(n - 1)
-                if n <= PASSES:
-                    load_piece(PROMPT, 1, n - 1)
-                if n == PASSES:
-                    load_bias(PROMPT)
+                if n == 1:
+                    load_piece(PROMPT, 1, 1)
             unit_on_vector(ahead - 1)
+            if u in BIAS_TURNS:
+                spread_bias(PROMPT, u - BIAS_TURNS[0])
             if u == 1:
                 for h in range(PASSES):
                     interleave_on_vector(

@@ -43,7 +43,7 @@ HEAD_UNITS = GROUPED_BUFS + QUANTISE_LEAD
 TENSOR_UNITS = (UNITS - 2, UNITS - 1)
 GPSIMD_UNITS = range(PASSES + 1 + HEAD_UNITS, LATE_UNIT + 2, PASSES)
 TENSOR_COLUMNS = [CHUNK if u in TENSOR_UNITS else 0 for u in range(UNITS)]
-GPSIMD_COLUMNS = [320 if u in GPSIMD_UNITS else 0 for u in range(UNITS)]
+GPSIMD_COLUMNS = [256 if u in GPSIMD_UNITS else 0 for u in range(UNITS)]
 VECTOR_COLUMNS = [256] * HEAD_UNITS + [16] * (LATE_UNIT - HEAD_UNITS) + [192] * 4 + [0] * 2
 BIAS_TURNS = (11, 12, 13)
 RESULT_BUFS = (5, 6)
@@ -329,13 +329,8 @@ def tile_block_pa_kernel(
                 for g in range(PASSES)
             ]
             nc.vector.memset(minus_half[:], -0.5)
-            half_row = TENSOR_WIDTH + CHUNK
-            nc.vector.memset(bias_rows[:, 0:half_row].bitcast(F32), 0.0)
-            nc.gpsimd.memset(bias_rows[:, half_row:OUT_WIDTH].bitcast(F32), 0.0)
             nc.scalar.activation(out=scratch[:], in_=minus_half[:], func=ACT.Identity)
-            nc.gpsimd.dma_start(out=bias_rows[0:1, :], in_=b_qkv.rearrange("(o n) -> o n", o=1))
-            nc.gpsimd.dma_start(out=bias_rows[32:33, :], in_=b_qkv_p.rearrange("(o n) -> o n", o=1))
-            nc.gpsimd.dma_start(out=x_class[:], in_=x[:, 0, :])
+            nc.scalar.dma_start(out=x_class[:], in_=x[:, 0, :])
             load_patch(x_patch, 2)
             load_piece(PATCH, 0, 0)
             load_patch(x_patch, 0)
@@ -351,6 +346,9 @@ def tile_block_pa_kernel(
                 nc.gpsimd.memset(pick[kind][32 * kind : 32 * kind + 32, :], 1.0)
             make_identity(nc, ident[:])
             make_identity(nc, ident_bf16[:])
+            nc.gpsimd.memset(bias_rows[:].bitcast(F32), 0.0)
+            nc.sync.dma_start(out=bias_rows[0:1, :], in_=b_qkv.rearrange("(o n) -> o n", o=1))
+            nc.sync.dma_start(out=bias_rows[32:33, :], in_=b_qkv_p.rearrange("(o n) -> o n", o=1))
             for v, vector in enumerate((n1_g, n1_b, n1p_g, n1p_b)):
                 nc.scalar.dma_start(
                     out=vectors[:, v, 0:PLANES].rearrange("p (g t) -> p g t", t=PACK),
@@ -358,8 +356,6 @@ def tile_block_pa_kernel(
                 )
 
             unit_on_scalar(0)
-            for third in range(3):
-                spread_bias(PATCH, third)
             patch_banks = [
                 psum.tile([P, TILES, P], F32, tag="bank", name="patch_bank_%d" % r)
                 for r in range(PLANES)
@@ -432,6 +428,8 @@ def tile_block_pa_kernel(
         unit_on_scalar(3)
         for r in range(PLANES):
             gain_on_scalar(p_planes[:, r, :], prompt_banks[r // PACK][:, r % PACK, :], 2, r)
+        for third in range(3):
+            spread_bias(PATCH, third)
         unit_on_scalar(4)
         unit_on_vector(3)
         unit_on_vector(4)

@@ -36,19 +36,16 @@ UNITS = 2 * CHUNKS * PASSES
 UNIT_KIND = [PATCH] * (CHUNKS * PASSES) + [PROMPT] * (CHUNKS * PASSES)
 PIECES = {PATCH: ((0, 1), (1, 2), (3, 3)), PROMPT: ((0, 3), (3, 3))}
 
-LATE_UNIT = 18
+LATE_UNIT = 20
 GROUPED_BUFS = 5
 QUANTISE_LEAD = 2
 HEAD_UNITS = GROUPED_BUFS + QUANTISE_LEAD
-TENSOR_UNITS = (UNITS - 2, UNITS - 1)
 GPSIMD_UNITS = range(PASSES + 1 + HEAD_UNITS, LATE_UNIT + 2, PASSES)
-TENSOR_COLUMNS = [CHUNK if u in TENSOR_UNITS else 0 for u in range(UNITS)]
-GPSIMD_COLUMNS = [256 if u in GPSIMD_UNITS else 0 for u in range(UNITS)]
-VECTOR_COLUMNS = [256] * HEAD_UNITS + [16] * (LATE_UNIT - HEAD_UNITS) + [192] * 4 + [0] * 2
+GPSIMD_COLUMNS = [320 if u in GPSIMD_UNITS else 0 for u in range(UNITS)]
+VECTOR_COLUMNS = [320] * HEAD_UNITS + [16] * (LATE_UNIT - HEAD_UNITS) + [128] * (UNITS - LATE_UNIT)
 BIAS_TURNS = (11, 12, 13)
 RESULT_BUFS = (5, 6)
 TOKENS_ON_VECTOR = 384
-BANK_COLUMNS = 256
 
 
 def tile_block_pa_kernel(
@@ -68,7 +65,6 @@ def tile_block_pa_kernel(
         minus_half = keep.tile([P, 2], F32)
         scratch = keep.tile([P, 2], F32)
         ident = keep.tile([P, P], F32)
-        ident_bf16 = keep.tile([P, P], BF16)
         x_class = keep.tile([SAMPLES, WIDTH], BF16)
         bias_rows = keep.tile([P, OUT_WIDTH], BF16)
         pick = {kind: keep.tile([P, P], BF16, name="pick_%d" % kind) for kind in KINDS}
@@ -227,25 +223,12 @@ def tile_block_pa_kernel(
                 )
                 lo = VECTOR_COLUMNS[u]
                 hi = lo + GPSIMD_COLUMNS[u]
-                end = CHUNK - TENSOR_COLUMNS[u]
                 if hi > lo:
                     interleave_on_gpsimd(grouped[u], weight(u), lo, hi)
-                for first in range(end, CHUNK, BANK_COLUMNS):
-                    bank = psum.tile([P, BANK_COLUMNS, PACK], BF16, tag="bank", name="group_bank")
-                    for c in range(0, BANK_COLUMNS, P):
-                        nc.tensor.matmul(
-                            out=bank[:, c : c + P, :].rearrange("p c t -> p t c"),
-                            lhsT=ident_bf16[:],
-                            rhs=weight(u)[:, :, first + c : first + c + P],
-                            start=True,
-                            stop=True,
-                        )
-                    nc.scalar.copy(out=grouped[u][:, first : first + BANK_COLUMNS, :], in_=bank[:])
-                if end > hi:
-                    interleave_on_scalar(grouped[u], weight(u), hi, end)
+                interleave_on_scalar(grouped[u], weight(u), hi, CHUNK)
 
         def unit_on_vector(u):
-            if u < UNITS and VECTOR_COLUMNS[u] > 0:
+            if u < UNITS:
                 interleave_on_vector(grouped[u], weight(u), 0, VECTOR_COLUMNS[u])
 
         def quantise_unit(u):
@@ -345,7 +328,6 @@ def tile_block_pa_kernel(
                 nc.gpsimd.memset(pick[kind][:].bitcast(F32), 0.0)
                 nc.gpsimd.memset(pick[kind][32 * kind : 32 * kind + 32, :], 1.0)
             make_identity(nc, ident[:])
-            make_identity(nc, ident_bf16[:])
             nc.gpsimd.memset(bias_rows[:].bitcast(F32), 0.0)
             nc.sync.dma_start(out=bias_rows[0:1, :], in_=b_qkv.rearrange("(o n) -> o n", o=1))
             nc.sync.dma_start(out=bias_rows[32:33, :], in_=b_qkv_p.rearrange("(o n) -> o n", o=1))
@@ -374,6 +356,7 @@ def tile_block_pa_kernel(
             half_statistics(3, x_patch[:, 3, :], 1)
             scales(2)
             patch_to_banks(2)
+            unit_on_scalar(1)
             half_statistics(1, x_patch[:, 1, :], 0)
             join_statistics(3)
             nc.vector.tensor_copy(out=x_patch[0:SAMPLES, 0, :], in_=x_class[:])
@@ -384,16 +367,15 @@ def tile_block_pa_kernel(
             join_statistics(1)
             half_statistics(0, x_patch[:, 0, :], 1)
             scales(1)
+            unit_on_scalar(2)
             patch_to_banks(1)
             unit_on_vector(0)
             join_statistics(0)
-            unit_on_scalar(1)
             unit_on_vector(1)
             scales(0)
             quantise_unit(0)
             patch_to_banks(0)
             nc.vector.tensor_copy(out=gain_shift[:], in_=vectors[:, :, 0:PLANES])
-            unit_on_scalar(2)
             half_statistics(TILES, x_prompt[:], 0)
             half_statistics(TILES, x_prompt[:], 1)
             unit_on_vector(2)

@@ -32,18 +32,21 @@ CHUNKS = OUT_WIDTH // CHUNK
 PATCH, PROMPT = 0, 1
 
 KINDS = (PATCH, PROMPT)
-UNITS = 2 * CHUNKS * PASSES
-UNIT_KIND = [PATCH] * (CHUNKS * PASSES) + [PROMPT] * (CHUNKS * PASSES)
-PIECES = {PATCH: ((0, 1), (1, 2), (3, 3)), PROMPT: ((0, 3), (3, 3))}
+PIECES = {PATCH: ((0, 1), (1, 1), (2, 4)), PROMPT: ((0, 3), (3, 3))}
+PROMPT_LOADS = [(which, g) for which in range(len(PIECES[PROMPT])) for g in range(PASSES)]
+EARLY_LOADS = 3
 
-LATE_UNIT = 20
-GROUPED_BUFS = 5
-QUANTISE_LEAD = 2
-HEAD_UNITS = GROUPED_BUFS + QUANTISE_LEAD
-GPSIMD_UNITS = range(PASSES + 1 + HEAD_UNITS, LATE_UNIT + 2, PASSES)
-GPSIMD_COLUMNS = [320 if u in GPSIMD_UNITS else 0 for u in range(UNITS)]
-VECTOR_COLUMNS = [320] * HEAD_UNITS + [16] * (LATE_UNIT - HEAD_UNITS) + [128] * (UNITS - LATE_UNIT)
-BIAS_TURNS = (11, 12, 13)
+PARTS = 2 * CHUNKS
+GROUPED_BUFS = 3
+VECTOR_LEAD = 3
+GPSIMD_PARTS = range(2 + GROUPED_BUFS, CHUNKS + 2 + GROUPED_BUFS)
+GPSIMD_COLUMNS = [(384 if n in GPSIMD_PARTS else 0, 0) for n in range(PARTS)]
+VECTOR_UNITS = ((0, 1), (2, 0), (2, 1), (3, 0))
+VECTOR_COLUMNS = [
+    [CHUNK if (n, g) in VECTOR_UNITS else 192 if n == PARTS - 1 else 0 for g in range(PASSES)]
+    for n in range(PARTS)
+]
+BIAS_TURNS = (3, 4, 5)
 RESULT_BUFS = (5, 6)
 TOKENS_ON_VECTOR = 384
 
@@ -58,7 +61,7 @@ def tile_block_pa_kernel(
     with ExitStack() as pools:
         keep = pools.enter_context(tc.tile_pool(name="keep", bufs=1))
         grouped_pool = pools.enter_context(tc.tile_pool(name="grouped", bufs=GROUPED_BUFS))
-        codes_pool = pools.enter_context(tc.tile_pool(name="codes", bufs=6))
+        codes_pool = pools.enter_context(tc.tile_pool(name="codes", bufs=3))
         psum = pools.enter_context(tc.psum_pool(name="psum", bufs=8))
         pools.enter_context(tc.manual_schedule())
 
@@ -212,59 +215,64 @@ def tile_block_pa_kernel(
         grouped = {}
         w_operand = {}
 
-        def weight(u):
-            chunk, g = divmod(u % (CHUNKS * PASSES), PASSES)
-            return raw[UNIT_KIND[u], chunk, g]
+        def weight(n, g):
+            return raw[n // CHUNKS, n % CHUNKS, g]
 
-        def unit_on_scalar(u):
-            if u < UNITS:
-                grouped[u] = grouped_pool.tile(
-                    [P, CHUNK, PACK], BF16, name="grouped", align_bytes=64
+        def unit_on_scalar(n, g):
+            if n >= PARTS:
+                return
+            if g == 0:
+                grouped[n] = grouped_pool.tile(
+                    [P, PASSES, CHUNK, PACK], BF16, name="grouped", align_bytes=64
                 )
-                lo = VECTOR_COLUMNS[u]
-                hi = lo + GPSIMD_COLUMNS[u]
-                if hi > lo:
-                    interleave_on_gpsimd(grouped[u], weight(u), lo, hi)
-                interleave_on_scalar(grouped[u], weight(u), hi, CHUNK)
+            lo = VECTOR_COLUMNS[n][g]
+            hi = lo + GPSIMD_COLUMNS[n][g]
+            if hi > lo:
+                interleave_on_gpsimd(grouped[n][:, g], weight(n, g), lo, hi)
+            if hi < CHUNK:
+                interleave_on_scalar(grouped[n][:, g], weight(n, g), hi, CHUNK)
 
-        def unit_on_vector(u):
-            if u < UNITS:
-                interleave_on_vector(grouped[u], weight(u), 0, VECTOR_COLUMNS[u])
+        def unit_on_vector(n, g):
+            if n < PARTS and VECTOR_COLUMNS[n][g] > 0:
+                interleave_on_vector(grouped[n][:, g], weight(n, g), 0, VECTOR_COLUMNS[n][g])
 
-        def quantise_unit(u):
-            if u < UNITS:
-                w_codes = codes_pool.tile([P, CHUNK], U32, name="w_codes", align_bytes=64)
-                w_scales = codes_pool.tile([P, CHUNK], U8, name="w_scales", align_bytes=64)
-                nc.vector.quantize_mx(
-                    out=w_codes[:].bitcast(FP8X4),
-                    scales=w_scales[:],
-                    in_=grouped[u][:].rearrange("p c t -> p (c t)"),
+        def quantise(n, first, last):
+            if n >= PARTS:
+                return
+            if first == 0:
+                w_operand[n] = (
+                    codes_pool.tile([P, PASSES, CHUNK], U32, name="w_codes", align_bytes=64),
+                    codes_pool.tile([P, PASSES, CHUNK], U8, name="w_scales", align_bytes=64),
                 )
-                w_operand[u] = (w_codes, w_scales)
+            w_codes, w_scales = w_operand[n]
+            passes = slice(first, last + 1)
+            nc.vector.quantize_mx(
+                out=w_codes[:, passes, :].rearrange("p g c -> p (g c)").bitcast(FP8X4),
+                scales=w_scales[:, passes, :].rearrange("p g c -> p (g c)"),
+                in_=grouped[n][:, passes].rearrange("p g c t -> p (g c t)"),
+            )
 
         acc = {}
 
-        def multiply_unit(u):
-            kind = UNIT_KIND[u]
-            chunk, g = divmod(u, PASSES)
+        def multiply_part(n):
             codes, code_scales, tiles = (
-                (x_codes, x_scales, TILES) if kind == PATCH else (p_codes, p_scales, 1)
+                (x_codes, x_scales, TILES) if n < CHUNKS else (p_codes, p_scales, 1)
             )
-            if g == 0:
-                acc[chunk] = [
-                    psum.tile([P, CHUNK], F32, tag="bank", name="acc_%d" % j) for j in range(tiles)
-                ]
-            w_codes, w_scales = w_operand[u]
-            for j in range(tiles):
-                nc.tensor.matmul_mx(
-                    out=acc[chunk][j][:],
-                    lhsT=codes[:, g, j * P : (j + 1) * P].bitcast(FP8X4),
-                    lhsT_scale=code_scales[:, g, j * P : (j + 1) * P],
-                    rhs=w_codes[:].bitcast(FP8X4),
-                    rhs_scale=w_scales[:],
-                    start=(g == 0),
-                    stop=(g == PASSES - 1),
-                )
+            acc[n] = [
+                psum.tile([P, CHUNK], F32, tag="bank", name="acc_%d" % j) for j in range(tiles)
+            ]
+            w_codes, w_scales = w_operand[n]
+            for g in range(PASSES):
+                for j in range(tiles):
+                    nc.tensor.matmul_mx(
+                        out=acc[n][j][:],
+                        lhsT=codes[:, g, j * P : (j + 1) * P].bitcast(FP8X4),
+                        lhsT_scale=code_scales[:, g, j * P : (j + 1) * P],
+                        rhs=w_codes[:, g, :].bitcast(FP8X4),
+                        rhs_scale=w_scales[:, g, :],
+                        start=(g == 0),
+                        stop=(g == PASSES - 1),
+                    )
 
         result = {}
 
@@ -322,8 +330,9 @@ def tile_block_pa_kernel(
             for b in range(SAMPLES):
                 nc.sync.dma_start(out=x_prompt[b:P:SAMPLES, :], in_=x[b, 1 : 1 + PROMPTS, :])
             load_piece(PATCH, 1, 1)
-            for g in range(PASSES):
-                load_piece(PATCH, 2, g)
+            for which in range(2, len(PIECES[PATCH])):
+                for g in range(PASSES):
+                    load_piece(PATCH, which, g)
             for kind in KINDS:
                 nc.gpsimd.memset(pick[kind][:].bitcast(F32), 0.0)
                 nc.gpsimd.memset(pick[kind][32 * kind : 32 * kind + 32, :], 1.0)
@@ -337,7 +346,7 @@ def tile_block_pa_kernel(
                     in_=vector.rearrange("(g p t) -> p g t", p=P, t=PACK),
                 )
 
-            unit_on_scalar(0)
+            unit_on_scalar(0, 0)
             patch_banks = [
                 psum.tile([P, TILES, P], F32, tag="bank", name="patch_bank_%d" % r)
                 for r in range(PLANES)
@@ -356,7 +365,7 @@ def tile_block_pa_kernel(
             half_statistics(3, x_patch[:, 3, :], 1)
             scales(2)
             patch_to_banks(2)
-            unit_on_scalar(1)
+            unit_on_scalar(0, 1)
             half_statistics(1, x_patch[:, 1, :], 0)
             join_statistics(3)
             nc.vector.tensor_copy(out=x_patch[0:SAMPLES, 0, :], in_=x_class[:])
@@ -367,20 +376,19 @@ def tile_block_pa_kernel(
             join_statistics(1)
             half_statistics(0, x_patch[:, 0, :], 1)
             scales(1)
-            unit_on_scalar(2)
+            unit_on_scalar(1, 0)
             patch_to_banks(1)
-            unit_on_vector(0)
+            unit_on_vector(0, 0)
             join_statistics(0)
-            unit_on_vector(1)
+            unit_on_vector(0, 1)
             scales(0)
-            quantise_unit(0)
+            quantise(0, 0, 1)
             patch_to_banks(0)
             nc.vector.tensor_copy(out=gain_shift[:], in_=vectors[:, :, 0:PLANES])
             half_statistics(TILES, x_prompt[:], 0)
             half_statistics(TILES, x_prompt[:], 1)
-            unit_on_vector(2)
+            unit_on_vector(1, 0)
             join_statistics(TILES)
-            quantise_unit(1)
             scales(TILES)
             z_prompt = z_pool.tile([P, PLANES, P], F32, name="z")
             normalise(z_prompt, TILES, x_prompt[:], False)
@@ -407,46 +415,56 @@ def tile_block_pa_kernel(
                     prompt_banks[r // PACK][:, r % PACK, :], z_prompt[:, r, :], ident[:]
                 )
         result_pool = pools.enter_context(tc.tile_pool(name="result", bufs=1))
-        unit_on_scalar(3)
+        unit_on_scalar(1, 1)
         for r in range(PLANES):
             gain_on_scalar(p_planes[:, r, :], prompt_banks[r // PACK][:, r % PACK, :], 2, r)
         for third in range(3):
             spread_bias(PATCH, third)
-        unit_on_scalar(4)
-        unit_on_vector(3)
-        unit_on_vector(4)
+        unit_on_scalar(2, 0)
+        unit_on_vector(1, 1)
+        unit_on_vector(2, 0)
+        for which, g in PROMPT_LOADS[:EARLY_LOADS]:
+            load_piece(PROMPT, which, g)
+        unit_on_scalar(2, 1)
+        unit_on_vector(2, 1)
         for g in range(PASSES):
-            load_piece(PROMPT, 0, g)
-        load_piece(PROMPT, 1, 0)
-        for u in range(GROUPED_BUFS, GROUPED_BUFS + QUANTISE_LEAD):
-            unit_on_scalar(u)
-        unit_on_vector(GROUPED_BUFS)
+            unit_on_scalar(3, g)
 
-        for u in range(UNITS):
-            n, g = divmod(u, PASSES)
-            ahead = u + QUANTISE_LEAD + GROUPED_BUFS
-            quantise_unit(u + QUANTISE_LEAD)
-            unit_on_scalar(ahead)
-            multiply_unit(u)
-            if n > 0 and g == 1:
-                for j in range(len(acc[n - 1])):
-                    add_bias(n - 1, j)
-                store(n - 1)
-                if n == 1:
-                    load_piece(PROMPT, 1, 1)
-            unit_on_vector(ahead - 1)
-            if u in BIAS_TURNS:
-                spread_bias(PROMPT, u - BIAS_TURNS[0])
-            if u == 1:
+        def finish(n):
+            for j in range(len(acc[n])):
+                add_bias(n, j)
+            store(n)
+
+        for n in range(PARTS):
+            late = n > CHUNKS
+            if late and n < PARTS - 1:
+                finish(n - 1)
+            if n < PARTS - 2:
+                quantise(n + 1, 0, 1)
+            for g in range(PASSES):
+                unit_on_scalar(n + 1 + GROUPED_BUFS, g)
+            multiply_part(n)
+            if n == PARTS - 2:
+                quantise(n + 1, 0, 0)
+                finish(n)
+                quantise(n + 1, 1, 1)
+            if n > 0 and not late:
+                finish(n - 1)
+                if n <= len(PROMPT_LOADS) - EARLY_LOADS:
+                    load_piece(PROMPT, *PROMPT_LOADS[EARLY_LOADS + n - 1])
+            for g in range(PASSES):
+                unit_on_vector(n + VECTOR_LEAD, g)
+            if n == 0:
                 for h in range(PASSES):
                     interleave_on_vector(
                         p_grouped[:, h], p_planes[:, PACK * h : PACK * (h + 1), :], 0, P
                     )
-            if u == 2:
+            if n == 1:
                 nc.vector.quantize_mx(
                     out=p_codes[:].rearrange("p g c -> p (g c)").bitcast(FP8X4),
                     scales=p_scales[:].rearrange("p g c -> p (g c)"),
                     in_=p_grouped[:].rearrange("p g c t -> p (g c t)"),
                 )
-        add_bias(2 * CHUNKS - 1, 0)
-        store(2 * CHUNKS - 1)
+            if n in BIAS_TURNS:
+                spread_bias(PROMPT, n - BIAS_TURNS[0])
+        finish(PARTS - 1)

from contextlib import ExitStack

import concourse.mybir as mybir
from concourse.masks import make_identity

F32 = mybir.dt.float32
BF16 = mybir.dt.bfloat16
U32 = mybir.dt.uint32
U8 = mybir.dt.uint8
FP8X4 = mybir.dt.float8_e4m3fn_x4
ACT = mybir.ActivationFunctionType
ALU = mybir.AluOpType

P = 128
PACK = 4
K_PASS = P * PACK
SAMPLES, TOKENS, WIDTH = 4, 160, 1024
PROMPTS = 32
HEADS, HEAD_DIM = 16, 64
TENSOR_WIDTH = HEADS * HEAD_DIM
OUT_WIDTH = 3 * TENSOR_WIDTH
PASSES = WIDTH // K_PASS
PLANES = WIDTH // P
EPS = 1e-5
FLOPS = 2 * SAMPLES * TOKENS * WIDTH * OUT_WIDTH

TILES = 4
CHUNK = 512
CHUNK_HEADS = CHUNK // HEAD_DIM
CHUNKS = OUT_WIDTH // CHUNK

PATCH, PROMPT = 0, 1

KINDS = (PATCH, PROMPT)
PIECES = {PATCH: ((0, 1), (1, 1), (2, 4)), PROMPT: ((0, 3), (3, 3))}
PROMPT_LOADS = [(which, g) for which in range(len(PIECES[PROMPT])) for g in range(PASSES)]
EARLY_LOADS = 3

PARTS = 2 * CHUNKS
GROUPED_BUFS = 3
VECTOR_LEAD = 3
GPSIMD_PARTS = range(2 + GROUPED_BUFS, CHUNKS + 2 + GROUPED_BUFS)
GPSIMD_COLUMNS = [(384 if n in GPSIMD_PARTS else 0, 0) for n in range(PARTS)]
VECTOR_UNITS = ((0, 1), (2, 0), (2, 1), (3, 0))
VECTOR_COLUMNS = [
    [CHUNK if (n, g) in VECTOR_UNITS else 192 if n == PARTS - 1 else 0 for g in range(PASSES)]
    for n in range(PARTS)
]
BIAS_TURNS = (3, 4, 5)
RESULT_BUFS = (5, 6)
TOKENS_ON_VECTOR = 384


def tile_block_pa_kernel(
    tc, x, w_qkv, b_qkv, w_qkv_p, b_qkv_p, n1_g, n1_b, n1p_g, n1p_b, out_0, out_1, out_2
):
    nc = tc.nc
    weights = {PATCH: w_qkv, PROMPT: w_qkv_p}
    outs = (out_0, out_1, out_2)

    with ExitStack() as pools:
        keep = pools.enter_context(tc.tile_pool(name="keep", bufs=1))
        grouped_pool = pools.enter_context(tc.tile_pool(name="grouped", bufs=GROUPED_BUFS))
        codes_pool = pools.enter_context(tc.tile_pool(name="codes", bufs=3))
        psum = pools.enter_context(tc.psum_pool(name="psum", bufs=8))
        pools.enter_context(tc.manual_schedule())

        minus_half = keep.tile([P, 2], F32)
        scratch = keep.tile([P, 2], F32)
        ident = keep.tile([P, P], F32)
        x_class = keep.tile([SAMPLES, WIDTH], BF16)
        bias_rows = keep.tile([P, OUT_WIDTH], BF16)
        pick = {kind: keep.tile([P, P], BF16, name="pick_%d" % kind) for kind in KINDS}
        vectors = keep.tile([P, 4, 2 * PLANES], BF16)
        gain_shift = keep.tile([P, 4, PLANES], F32)
        x_prompt = keep.tile([P, WIDTH], BF16)
        stats = keep.tile([P, TILES + 1, 2, 6], F32)
        mean_var = keep.tile([P, TILES + 1, 2], F32)
        var_eps = keep.tile([P, TILES + 1], F32)
        rstd = keep.tile([P, TILES + 1], F32)
        minus_mean = keep.tile([P, TILES + 1], F32)
        minus_mean_rstd = keep.tile([P, TILES + 1], F32)
        x_codes = keep.tile([P, PASSES, TILES * P], U32, align_bytes=64)
        x_scales = keep.tile([P, PASSES, TILES * P], U8, align_bytes=64)
        p_planes = keep.tile([P, PLANES, P], BF16)
        p_grouped = keep.tile([P, PASSES, P, PACK], BF16, align_bytes=64)
        p_codes = keep.tile([P, PASSES, P], U32, align_bytes=64)
        p_scales = keep.tile([P, PASSES, P], U8, align_bytes=64)

        def load_patch(x_patch, j):
            for b in range(SAMPLES):
                nc.sync.dma_start(
                    out=x_patch[b:P:SAMPLES, j : j + 2, :],
                    in_=x[b, PROMPTS:TOKENS, :].rearrange("(i j) c -> i j c", j=TILES)[
                        :, j : j + 2, :
                    ],
                )

        raw = {}

        def load_piece(kind, which, g):
            first, chunks = PIECES[kind][which]
            piece = keep.tile([P, PACK, chunks * CHUNK], BF16, name="raw_%d_%d_%d" % (kind, which, g))
            nc.sync.dma_start(
                out=piece[:],
                in_=weights[kind].rearrange("(g p t) n -> g p t n", p=P, t=PACK)[
                    g, :, :, first * CHUNK : (first + chunks) * CHUNK
                ],
            )
            for c in range(chunks):
                raw[kind, first + c, g] = piece[:, :, c * CHUNK : (c + 1) * CHUNK]

        bias = {
            kind: keep.tile([P, OUT_WIDTH], BF16, name="bias_%d" % kind) for kind in KINDS
        }

        def spread_bias(kind, third):
            bank = psum.tile([P, TENSOR_WIDTH], BF16, tag="bank", name="bias_bank")
            for half in range(2):
                first = third * TENSOR_WIDTH + half * CHUNK
                nc.tensor.matmul(
                    out=bank[:, half * CHUNK : (half + 1) * CHUNK],
                    lhsT=pick[kind][:],
                    rhs=bias_rows[:, first : first + CHUNK],
                    start=True,
                    stop=True,
                )
            nc.scalar.copy(
                out=bias[kind][:, third * TENSOR_WIDTH : (third + 1) * TENSOR_WIDTH], in_=bank[:]
            )

        def half_statistics(a, rows, half):
            nc.vector.bn_stats(
                out=stats[:, a, half, :], in_=rows[:, half * K_PASS : (half + 1) * K_PASS]
            )

        def join_statistics(a):
            nc.vector.bn_aggr(
                out=mean_var[:, a, :], in_=stats[:, a, :, :].rearrange("p h s -> p (h s)")
            )

        def scales(a):
            col = slice(a, a + 1)
            nc.vector.tensor_scalar_add(out=var_eps[:, col], in0=mean_var[:, a, 1:2], scalar1=EPS)
            nc.vector.tensor_scalar_mul(out=minus_mean[:, col], in0=mean_var[:, a, 0:1], scalar1=-1.0)
            nc.gpsimd.tensor_tensor(
                out=rstd[:, col], in0=var_eps[:, col], in1=minus_half[:, 0:1], op=ALU.pow
            )
            nc.gpsimd.tensor_tensor(
                out=minus_mean_rstd[:, col], in0=minus_mean[:, col], in1=rstd[:, col], op=ALU.mult
            )

        def normalise(z, a, rows, on_scalar):
            out = z[:].rearrange("q (g t) p -> q g t p", t=PACK)
            in_ = rows.rearrange("q (g p t) -> q g t p", p=P, t=PACK)
            if on_scalar:
                nc.scalar.activation(
                    out=out,
                    in_=in_,
                    func=ACT.Identity,
                    scale=rstd[:, a : a + 1],
                    bias=minus_mean_rstd[:, a : a + 1],
                )
            else:
                nc.gpsimd.tensor_scalar(
                    out=out,
                    in0=in_,
                    scalar1=rstd[:, a : a + 1],
                    scalar2=minus_mean_rstd[:, a : a + 1],
                    op0=ALU.mult,
                    op1=ALU.add,
                )

        def gain_on_scalar(out, bank, vector, r):
            nc.scalar.activation(
                out=out,
                in_=bank,
                func=ACT.Identity,
                scale=gain_shift[:, vector, r : r + 1],
                bias=gain_shift[:, vector + 1, r : r + 1],
            )

        def gain_on_vector(out, bank, vector, r):
            nc.vector.tensor_scalar(
                out=out,
                in0=bank,
                scalar1=gain_shift[:, vector, r : r + 1],
                scalar2=gain_shift[:, vector + 1, r : r + 1],
                op0=ALU.mult,
                op1=ALU.add,
            )

        def interleave_on_vector(dst, src, lo, hi):
            nc.vector.tensor_copy(
                out=dst[:, lo:hi, :].rearrange("p (c i) t -> p c t i", i=4),
                in_=src[:, :, lo:hi].rearrange("p t (c i) -> p c t i", i=4),
            )

        def interleave_on_scalar(dst, src, lo, hi):
            nc.scalar.copy(
                out=dst[:, lo:hi, :].rearrange("p (c i) t -> p c t i", i=4),
                in_=src[:, :, lo:hi].rearrange("p t (c i) -> p c t i", i=4),
            )

        def interleave_on_gpsimd(dst, src, lo, hi):
            nc.gpsimd.tensor_scalar(
                out=dst[:, lo:hi, :],
                in0=src[:, :, lo:hi].rearrange("p t c -> p c t"),
                scalar1=1.0,
                scalar2=0.0,
                op0=ALU.mult,
                op1=ALU.add,
            )

        grouped = {}
        w_operand = {}

        def weight(n, g):
            return raw[n // CHUNKS, n % CHUNKS, g]

        def unit_on_scalar(n, g):
            if n >= PARTS:
                return
            if g == 0:
                grouped[n] = grouped_pool.tile(
                    [P, PASSES, CHUNK, PACK], BF16, name="grouped", align_bytes=64
                )
            lo = VECTOR_COLUMNS[n][g]
            hi = lo + GPSIMD_COLUMNS[n][g]
            if hi > lo:
                interleave_on_gpsimd(grouped[n][:, g], weight(n, g), lo, hi)
            if hi < CHUNK:
                interleave_on_scalar(grouped[n][:, g], weight(n, g), hi, CHUNK)

        def unit_on_vector(n, g):
            if n < PARTS and VECTOR_COLUMNS[n][g] > 0:
                interleave_on_vector(grouped[n][:, g], weight(n, g), 0, VECTOR_COLUMNS[n][g])

        def quantise(n, first, last):
            if n >= PARTS:
                return
            if first == 0:
                w_operand[n] = (
                    codes_pool.tile([P, PASSES, CHUNK], U32, name="w_codes", align_bytes=64),
                    codes_pool.tile([P, PASSES, CHUNK], U8, name="w_scales", align_bytes=64),
                )
            w_codes, w_scales = w_operand[n]
            passes = slice(first, last + 1)
            nc.vector.quantize_mx(
                out=w_codes[:, passes, :].rearrange("p g c -> p (g c)").bitcast(FP8X4),
                scales=w_scales[:, passes, :].rearrange("p g c -> p (g c)"),
                in_=grouped[n][:, passes].rearrange("p g c t -> p (g c t)"),
            )

        acc = {}

        def multiply_part(n):
            codes, code_scales, tiles = (
                (x_codes, x_scales, TILES) if n < CHUNKS else (p_codes, p_scales, 1)
            )
            acc[n] = [
                psum.tile([P, CHUNK], F32, tag="bank", name="acc_%d" % j) for j in range(tiles)
            ]
            w_codes, w_scales = w_operand[n]
            for g in range(PASSES):
                for j in range(tiles):
                    nc.tensor.matmul_mx(
                        out=acc[n][j][:],
                        lhsT=codes[:, g, j * P : (j + 1) * P].bitcast(FP8X4),
                        lhsT_scale=code_scales[:, g, j * P : (j + 1) * P],
                        rhs=w_codes[:, g, :].bitcast(FP8X4),
                        rhs_scale=w_scales[:, g, :],
                        start=(g == 0),
                        stop=(g == PASSES - 1),
                    )

        result = {}

        def add_bias(n, j):
            kind, chunk = divmod(n, CHUNKS)
            if j == 0:
                result[n] = result_pool.tile(
                    [P, CHUNK_HEADS, len(acc[n]), HEAD_DIM],
                    F32,
                    name="result_%d" % kind,
                    bufs=RESULT_BUFS[kind],
                )
            nc.vector.tensor_tensor(
                out=result[n][:, :, j, :],
                in0=acc[n][j][:].rearrange("p (h d) -> p h d", d=HEAD_DIM),
                in1=bias[kind][:, chunk * CHUNK : (chunk + 1) * CHUNK].rearrange(
                    "p (h d) -> p h d", d=HEAD_DIM
                ),
                op=ALU.add,
            )

        def store(n):
            kind, chunk = divmod(n, CHUNKS)
            third, half = divmod(chunk, 2)
            heads = outs[third][:, half * CHUNK_HEADS : (half + 1) * CHUNK_HEADS, :, :]
            for b in range(SAMPLES):
                if kind == PATCH:
                    nc.sync.dma_start(
                        out=heads[b, :, PROMPTS:TOKENS, :].rearrange("h (i j) d -> i h (j d)", j=TILES),
                        in_=result[n][b:P:SAMPLES].rearrange("p h j d -> p h (j d)"),
                    )
                else:
                    nc.sync.dma_start(
                        out=heads[b, :, 1 : 1 + PROMPTS, :].rearrange("h m d -> m h d"),
                        in_=result[n][b:P:SAMPLES, :, 0, :],
                    )
            if kind == PATCH:
                nc.sync.dma_start(out=heads[:, :, 0, :], in_=result[n][0:SAMPLES, :, 0, :])

        with tc.tile_pool(name="head", bufs=1) as head, tc.tile_pool(name="z", bufs=3) as z_pool:
            x_patch = head.tile([P, TILES, WIDTH], BF16)
            x_planes = head.tile([P, PLANES, TILES * P], BF16)
            x_grouped = [
                head.tile([P, CHUNK, PACK], BF16, name="x_grouped_%d" % g, align_bytes=64)
                for g in range(PASSES)
            ]
            nc.vector.memset(minus_half[:], -0.5)
            nc.scalar.activation(out=scratch[:], in_=minus_half[:], func=ACT.Identity)
            nc.scalar.dma_start(out=x_class[:], in_=x[:, 0, :])
            load_patch(x_patch, 2)
            load_piece(PATCH, 0, 0)
            load_patch(x_patch, 0)
            load_piece(PATCH, 0, 1)
            load_piece(PATCH, 1, 0)
            for b in range(SAMPLES):
                nc.sync.dma_start(out=x_prompt[b:P:SAMPLES, :], in_=x[b, 1 : 1 + PROMPTS, :])
            load_piece(PATCH, 1, 1)
            for which in range(2, len(PIECES[PATCH])):
                for g in range(PASSES):
                    load_piece(PATCH, which, g)
            for kind in KINDS:
                nc.gpsimd.memset(pick[kind][:].bitcast(F32), 0.0)
                nc.gpsimd.memset(pick[kind][32 * kind : 32 * kind + 32, :], 1.0)
            make_identity(nc, ident[:])
            nc.gpsimd.memset(bias_rows[:].bitcast(F32), 0.0)
            nc.sync.dma_start(out=bias_rows[0:1, :], in_=b_qkv.rearrange("(o n) -> o n", o=1))
            nc.sync.dma_start(out=bias_rows[32:33, :], in_=b_qkv_p.rearrange("(o n) -> o n", o=1))
            for v, vector in enumerate((n1_g, n1_b, n1p_g, n1p_b)):
                nc.scalar.dma_start(
                    out=vectors[:, v, 0:PLANES].rearrange("p (g t) -> p g t", t=PACK),
                    in_=vector.rearrange("(g p t) -> p g t", p=P, t=PACK),
                )

            unit_on_scalar(0, 0)
            patch_banks = [
                psum.tile([P, TILES, P], F32, tag="bank", name="patch_bank_%d" % r)
                for r in range(PLANES)
            ]

            def patch_to_banks(a):
                z = z_pool.tile([P, PLANES, P], F32, name="z")
                normalise(z, a, x_patch[:, a, :], True)
                for r in range(PLANES):
                    nc.tensor.transpose(patch_banks[r][:, a, :], z[:, r, :], ident[:])

            half_statistics(2, x_patch[:, 2, :], 0)
            half_statistics(2, x_patch[:, 2, :], 1)
            half_statistics(3, x_patch[:, 3, :], 0)
            join_statistics(2)
            half_statistics(3, x_patch[:, 3, :], 1)
            scales(2)
            patch_to_banks(2)
            unit_on_scalar(0, 1)
            half_statistics(1, x_patch[:, 1, :], 0)
            join_statistics(3)
            nc.vector.tensor_copy(out=x_patch[0:SAMPLES, 0, :], in_=x_class[:])
            scales(3)
            patch_to_banks(3)
            half_statistics(1, x_patch[:, 1, :], 1)
            half_statistics(0, x_patch[:, 0, :], 0)
            join_statistics(1)
            half_statistics(0, x_patch[:, 0, :], 1)
            scales(1)
            unit_on_scalar(1, 0)
            patch_to_banks(1)
            unit_on_vector(0, 0)
            join_statistics(0)
            unit_on_vector(0, 1)
            scales(0)
            quantise(0, 0, 1)
            patch_to_banks(0)
            nc.vector.tensor_copy(out=gain_shift[:], in_=vectors[:, :, 0:PLANES])
            half_statistics(TILES, x_prompt[:], 0)
            half_statistics(TILES, x_prompt[:], 1)
            unit_on_vector(1, 0)
            join_statistics(TILES)
            scales(TILES)
            z_prompt = z_pool.tile([P, PLANES, P], F32, name="z")
            normalise(z_prompt, TILES, x_prompt[:], False)
            for r in range(PLANES):
                (gain_on_scalar if r % PACK < 2 else gain_on_vector)(
                    x_planes[:, r, :], patch_banks[r][:].rearrange("p j c -> p (j c)"), 0, r
                )
            for g in range(PASSES):
                planes = x_planes[:, PACK * g : PACK * (g + 1), :]
                interleave_on_scalar(x_grouped[g], planes, TOKENS_ON_VECTOR, CHUNK)
                interleave_on_vector(x_grouped[g], planes, 0, TOKENS_ON_VECTOR)
            for g in range(PASSES):
                nc.vector.quantize_mx(
                    out=x_codes[:, g, :].bitcast(FP8X4),
                    scales=x_scales[:, g, :],
                    in_=x_grouped[g][:].rearrange("p c t -> p (c t)"),
                )
            prompt_banks = [
                psum.tile([P, PACK, P], F32, tag="bank", name="prompt_bank_%d" % g)
                for g in range(PASSES)
            ]
            for r in range(PLANES):
                nc.tensor.transpose(
                    prompt_banks[r // PACK][:, r % PACK, :], z_prompt[:, r, :], ident[:]
                )
        result_pool = pools.enter_context(tc.tile_pool(name="result", bufs=1))
        unit_on_scalar(1, 1)
        for r in range(PLANES):
            gain_on_scalar(p_planes[:, r, :], prompt_banks[r // PACK][:, r % PACK, :], 2, r)
        for third in range(3):
            spread_bias(PATCH, third)
        unit_on_scalar(2, 0)
        unit_on_vector(1, 1)
        unit_on_vector(2, 0)
        for which, g in PROMPT_LOADS[:EARLY_LOADS]:
            load_piece(PROMPT, which, g)
        unit_on_scalar(2, 1)
        unit_on_vector(2, 1)
        for g in range(PASSES):
            unit_on_scalar(3, g)

        def finish(n):
            for j in range(len(acc[n])):
                add_bias(n, j)
            store(n)

        for n in range(PARTS):
            late = n > CHUNKS
            if late and n < PARTS - 1:
                finish(n - 1)
            if n < PARTS - 2:
                quantise(n + 1, 0, 1)
            for g in range(PASSES):
                unit_on_scalar(n + 1 + GROUPED_BUFS, g)
            multiply_part(n)
            if n == PARTS - 2:
                quantise(n + 1, 0, 0)
                finish(n)
                quantise(n + 1, 1, 1)
            if n > 0 and not late:
                finish(n - 1)
                if n <= len(PROMPT_LOADS) - EARLY_LOADS:
                    load_piece(PROMPT, *PROMPT_LOADS[EARLY_LOADS + n - 1])
            for g in range(PASSES):
                unit_on_vector(n + VECTOR_LEAD, g)
            if n == 0:
                for h in range(PASSES):
                    interleave_on_vector(
                        p_grouped[:, h], p_planes[:, PACK * h : PACK * (h + 1), :], 0, P
                    )
            if n == 1:
                nc.vector.quantize_mx(
                    out=p_codes[:].rearrange("p g c -> p (g c)").bitcast(FP8X4),
                    scales=p_scales[:].rearrange("p g c -> p (g c)"),
                    in_=p_grouped[:].rearrange("p g c t -> p (g c t)"),
                )
            if n in BIAS_TURNS:
                spread_bias(PROMPT, n - BIAS_TURNS[0])
        finish(PARTS - 1)
